import numpy as np
import ml_dtypes


def mxq(x, axis, fmt="e4m3"):
    dtype, down = {"e4m3": (ml_dtypes.float8_e4m3fn, 7), "e5m2": (ml_dtypes.float8_e5m2, 14)}[fmt]
    v = np.moveaxis(np.asarray(x, np.float32).astype(ml_dtypes.bfloat16).astype(np.float64), axis, -1)
    blocks = v.reshape(v.shape[:-1] + (-1, 32))
    amax = np.abs(blocks).max(-1, keepdims=True)
    byte = np.maximum(np.where(amax > 0, np.frexp(amax)[1] - 1 + 127, 0) - down, 1)
    scale = np.exp2(byte - 127.0)
    codes = (blocks / scale).astype(np.float32).astype(dtype).astype(np.float64)
    return np.moveaxis((codes * scale).reshape(v.shape), -1, axis)


WIDE = False


def mx_kscale(k):
    if not WIDE:
        return np.ones(k)
    levels = np.array([10, -10, 5, -5, 0])
    a = np.random.permutation(np.resize(levels, k // 512 * 4)).reshape(k // 512, 4)
    idx = np.arange(k)
    return np.exp2(a[idx // 512, idx % 128 // 32])


BF16 = ml_dtypes.bfloat16


def bf(x):
    return np.asarray(x, np.float32).astype(BF16)


def f64(x):
    return np.asarray(x).astype(np.float64)


N, C, D, H, W, GD, GH, GW, FD, FH, FW = 2, 512, 8, 16, 8, 8, 8, 8, 4, 8, 8
V = D * H * W
G = GD * GH * GW
PD, PH, PW = D // GD, H // GH, W // GW


def erf(z):
    a = np.minimum(np.abs(z), 6.0)
    q = 2.0 * a * a
    t = a.copy()
    s = a.copy()
    n = 0
    while np.any(t > 1e-18 * s):
        n += 1
        t = t * q / (2 * n + 1)
        s = s + t
    return np.sign(z) * (2.0 / np.sqrt(np.pi)) * np.exp(-a * a) * s


def gelu(t):
    return 0.5 * t * (1.0 + erf(t / np.sqrt(2.0)))


def block(t, ps):
    n, c, d, h, w = t.shape
    t = t.reshape(n, c, d // ps[0], ps[0], h // ps[1], ps[1], w // ps[2], ps[2])
    return t.transpose(0, 1, 2, 4, 6, 3, 5, 7).reshape(n, c, -1, ps[0] * ps[1] * ps[2])


def unblock(t, gs, ps):
    n, c = t.shape[:2]
    t = t.reshape(n, c, gs[0], gs[1], gs[2], ps[0], ps[1], ps[2]).transpose(0, 1, 2, 5, 3, 6, 4, 7)
    return t.reshape(n, c, gs[0] * ps[0], gs[1] * ps[1], gs[2] * ps[2])


def setup_inputs():
    s = mx_kscale(C)
    return {"x_norm": bf(np.random.standard_normal((N, C, D, H, W)) * s[None, :, None, None, None]),
            "w1_u": bf(np.random.standard_normal((C, C)) / np.sqrt(C) / s[None, :]),
            "b1_u": bf(np.random.standard_normal(C) * 0.3),
            "w2": bf(np.random.standard_normal((G, G)) / np.sqrt(G)),
            "b2": bf(np.random.standard_normal(G) * 0.3)}


def reference(x_norm, w1_u, b1_u, w2, b2):
    z = mxq(f64(w1_u), 1, "e4m3") @ mxq(f64(x_norm).reshape(N, C, V), 1, "e4m3")
    u = gelu(z + f64(b1_u)[None, :, None]).reshape(N, C, D, H, W)
    u = block(u, (PD, PH, PW))
    y = (mxq(f64(w2), 1, "e4m3") @ mxq(u, 2, "e4m3")) + f64(b2)[None, None, :, None]
    return unblock(y, (GD, GH, GW), (PD, PH, PW))

@@ -1,0 +1,273 @@
+from contextlib import ExitStack
+
+import concourse.mybir as mybir
+from concourse.masks import make_identity
+
+F32 = mybir.dt.float32
+BF16 = mybir.dt.bfloat16
+U32 = mybir.dt.uint32
+U8 = mybir.dt.uint8
+FP8X4 = mybir.dt.float8_e4m3fn_x4
+ACT = mybir.ActivationFunctionType
+ALU = mybir.AluOpType
+
+P = 128
+FLOPS = 2 * 2 * 512 * 512 * 1024 * 2
+PIN = False
+UEVAC_ON_VECTOR = ()
+
+
+def tile_getspatialgatingweights_pa_kernel(tc, x_norm, w1_u, b1_u, w2, b2, out):
+    nc = tc.nc
+    with ExitStack() as ctx:
+        const = ctx.enter_context(tc.tile_pool(name="const", bufs=1))
+        upool = ctx.enter_context(tc.tile_pool(name="upool", bufs=3))
+        opool = ctx.enter_context(tc.tile_pool(name="opool", bufs=4))
+        zps = ctx.enter_context(tc.psum_pool(name="zps", bufs=3))
+        tps = ctx.enter_context(tc.psum_pool(name="tps", bufs=2))
+        yps = ctx.enter_context(tc.psum_pool(name="yps", bufs=3))
+        if PIN:
+            ctx.enter_context(tc.manual_schedule())
+
+        xv = x_norm.rearrange("n (u q e) d h w -> n u q e (d h w)", u=2, e=2)
+        w1v = w1_u.rearrange("(m a) c -> m a c", a=4)
+        w2v = w2.rearrange("(b m) g -> m b g", m=P)
+        ov = out.rearrange("n (m a) d h w -> n a m (d h w)", a=4)
+
+        identf = const.tile([P, P], F32, name="identf")
+        identb = const.tile([P, P], BF16, name="identb")
+        ones = const.tile([P, P], BF16, name="ones")
+        bz = const.tile([P, 512], BF16, name="bz")
+        b2bc = const.tile([P, 512], F32, name="b2bc")
+        b1bf = const.tile([P, 4], BF16, name="b1bf")
+        b1f = const.tile([P, 4], F32, name="b1f")
+        warm = const.tile([P, 1], F32, name="warm")
+        warm2 = const.tile([P, 1], F32, name="warm2")
+        w1sb = const.tile([P, 2048], BF16, name="w1sb")
+        w2sb = const.tile([P, 2048], BF16, name="w2sb")
+        w1g = const.tile([P, 2048], BF16, name="w1g", align_bytes=64)
+        w2g = const.tile([P, 2048], BF16, name="w2g", align_bytes=64)
+        w1c = const.tile([P, 512], U32, name="w1c", align_bytes=64)
+        w1s = const.tile([P, 512], U8, name="w1s", align_bytes=64)
+        w2c = const.tile([P, 512], U32, name="w2c", align_bytes=64)
+        w2s = const.tile([P, 512], U8, name="w2s", align_bytes=64)
+        xsb = [const.tile([P, 4096], BF16, name="xsb%d" % n) for n in range(2)]
+        xg = [const.tile([P, 2048], BF16, name="xg%d" % k, align_bytes=64) for k in range(4)]
+        xc = [const.tile([P, 512], U32, name="xc%d" % k, align_bytes=64) for k in range(4)]
+        xs = [const.tile([P, 512], U8, name="xs%d" % k, align_bytes=64) for k in range(4)]
+
+        nc.scalar.dma_start(out=b1bf[:], in_=b1_u.rearrange("(m a) -> m a", a=4))
+        nc.gpsimd.memset(bz[:], 0.0)
+        nc.scalar.dma_start(out=bz[0:1, :], in_=b2.rearrange("(o k) -> o k", o=1))
+        nc.sync.dma_start(out=w1sb[:, 0:512], in_=w1v[:, 0, :])
+        for hf in range(2):
+            for u in range(2):
+                nc.sync.dma_start(
+                    out=xsb[0][:].rearrange("q (t v) -> q t v", t=4)[:, 2 * u:2 * u + 2, hf * 512:(hf + 1) * 512],
+                    in_=xv[0, u][:, :, hf * 512:(hf + 1) * 512],
+                )
+        nc.sync.dma_start(out=w1sb[:, 512:2048].rearrange("m (a c) -> m a c", a=3), in_=w1v[:, 1:4, :])
+        nc.sync.dma_start(out=w2sb[:].rearrange("m (b g) -> m b g", b=4), in_=w2v)
+        for u in range(2):
+            nc.sync.dma_start(
+                out=xsb[1][:, 2 * u * 1024:(2 * u + 2) * 1024].rearrange("q (e v) -> q e v", e=2),
+                in_=xv[1, u],
+            )
+
+        make_identity(nc, identf[:])
+        nc.gpsimd.memset(ones[:], 1.0)
+        make_identity(nc, identb[:])
+        nc.vector.memset(warm[:], 0.0)
+        nc.scalar.activation(out=warm2[:], in_=warm[:], func=ACT.Gelu)
+        nc.vector.tensor_copy(out=b1f[:], in_=b1bf[:])
+
+        w1words = w1sb[:].bitcast(F32)
+        w1gwords = w1g[:].bitcast(F32)
+
+        def w1_tile(a, pool, tag):
+            pw = pool.tile([P, 256], F32, name="pw%d" % a, tag=tag)
+            for u in range(2):
+                nc.tensor.transpose(
+                    out=pw[:, u * P:(u + 1) * P],
+                    in_=w1words[:, a * 256 + u * P:a * 256 + (u + 1) * P],
+                    identity=identf[:],
+                )
+            nc.vector.tensor_copy(
+                out=w1gwords[:, a * 256:(a + 1) * 256].rearrange("q (m u) -> q m u", u=2),
+                in_=pw[:].rearrange("q (u m) -> q m u", u=2),
+            )
+
+        def w1_quant(a):
+            nc.vector.quantize_mx(
+                out=w1c[:, a * P:(a + 1) * P].bitcast(FP8X4),
+                scales=w1s[:, a * P:(a + 1) * P],
+                in_=w1g[:, a * 512:(a + 1) * 512],
+            )
+
+        def x_regroup(n, ph, hf, on_scalar):
+            k = 2 * n + ph
+            s0, s1 = hf * 32, (hf + 1) * 32
+            if on_scalar:
+                nc.scalar.copy(
+                    out=xg[k][:].rearrange("q (s i t) -> q s i t", i=8, t=4)[:, s0:s1],
+                    in_=xsb[n][:].rearrange("q (t s h i) -> q h s i t", t=4, h=2, i=8)[:, ph, s0:s1],
+                )
+            else:
+                nc.vector.tensor_copy(
+                    out=xg[k][:].rearrange("q (s i t) -> q s t i", i=8, t=4)[:, s0:s1],
+                    in_=xsb[n][:].rearrange("q (t s h i) -> q h s t i", t=4, h=2, i=8)[:, ph, s0:s1],
+                )
+
+        def x_quant(n, ph):
+            k = 2 * n + ph
+            nc.vector.quantize_mx(out=xc[k][:].bitcast(FP8X4), scales=xs[k][:], in_=xg[k][:])
+
+        zt = {}
+        usb = {}
+        utp = {}
+        ugt = {}
+        uct = {}
+        ust = {}
+        yt = {}
+        osb = {}
+
+        def mx1(j, ph):
+            n, a = j // 4, j % 4
+            z = zps.tile([P, 512], F32, name="z%d_%d" % (j, ph), tag="z")
+            zt[(j, ph)] = z
+            nc.tensor.matmul_mx(
+                out=z[:],
+                lhsT=w1c[:, a * P:(a + 1) * P].bitcast(FP8X4),
+                lhsT_scale=w1s[:, a * P:(a + 1) * P],
+                rhs=xc[2 * n + ph][:].bitcast(FP8X4),
+                rhs_scale=xs[2 * n + ph][:],
+                start=True,
+                stop=True,
+            )
+
+        def gelu(j):
+            a = j % 4
+            u_sb = upool.tile([P, 1024], BF16, name="usb%d" % j, tag="usb")
+            usb[j] = u_sb
+            for ph in range(2):
+                nc.scalar.activation(
+                    out=u_sb[:, ph * 512:(ph + 1) * 512],
+                    in_=zt[(j, ph)][:],
+                    func=ACT.Gelu,
+                    bias=b1f[:, a:a + 1],
+                    scale=1.0,
+                )
+
+        def tr(j):
+            ut = tps.tile([P, 1024], BF16, name="ut%d" % j, tag="t")
+            utp[j] = ut
+            for k in range(8):
+                nc.tensor.transpose(
+                    out=ut[:, k * P:(k + 1) * P],
+                    in_=usb[j][:, k * P:(k + 1) * P],
+                    identity=identb[:],
+                )
+
+        def uevac(j):
+            ug = upool.tile([P, 1024], BF16, name="ug%d" % j, tag="ug", align_bytes=64)
+            ugt[j] = ug
+            dst = ug[:].rearrange("p (h m t) -> p h m t", h=2, t=4)
+            srcv = utp[j][:].rearrange("p (h t m) -> p h m t", h=2, t=4)
+            if j in UEVAC_ON_VECTOR:
+                nc.vector.tensor_copy(out=dst, in_=srcv)
+            else:
+                nc.scalar.copy(out=dst, in_=srcv)
+
+        def uquant(j):
+            uc = upool.tile([P, 256], U32, name="uc%d" % j, tag="uc", align_bytes=64)
+            us = upool.tile([P, 256], U8, name="us%d" % j, tag="us", align_bytes=64)
+            uct[j] = uc
+            ust[j] = us
+            nc.vector.quantize_mx(out=uc[:].bitcast(FP8X4), scales=us[:], in_=ugt[j][:])
+
+        def mx2(j):
+            for ph in range(2):
+                y = yps.tile([P, 512], F32, name="y%d_%d" % (j, ph), tag="y")
+                yt[(j, ph)] = y
+                nc.tensor.matmul_mx(
+                    out=y[:],
+                    lhsT=uct[j][:, ph * P:(ph + 1) * P].bitcast(FP8X4),
+                    lhsT_scale=ust[j][:, ph * P:(ph + 1) * P],
+                    rhs=w2c[:].bitcast(FP8X4),
+                    rhs_scale=w2s[:],
+                    start=True,
+                    stop=True,
+                )
+
+        def yevac(j):
+            n, a = j // 4, j % 4
+            o_sb = opool.tile([P, 1024], F32, name="osb%d" % j, tag="osb")
+            osb[j] = o_sb
+            for ph in range(2):
+                nc.vector.tensor_tensor(
+                    out=o_sb[:].rearrange("m (s h i) -> m h s i", h=2, i=8)[:, ph],
+                    in0=yt[(j, ph)][:].rearrange("m (s i) -> m s i", i=8),
+                    in1=b2bc[:].rearrange("m (s i) -> m s i", i=8),
+                    op=ALU.add,
+                )
+            nc.sync.dma_start(out=ov[n, a], in_=o_sb[:])
+
+        w1_tile(0, yps, "y")
+        pb = tps.tile([P, 512], F32, name="pb", tag="t")
+        nc.tensor.matmul(out=pb[:], lhsT=ones[:], rhs=bz[:], start=True, stop=True)
+        nc.scalar.copy(out=b2bc[:], in_=pb[:])
+        x_regroup(0, 0, 0, False)
+        x_regroup(0, 1, 0, True)
+        w1_quant(0)
+        x_regroup(0, 0, 1, False)
+        x_regroup(0, 1, 1, True)
+        x_quant(0, 0)
+        x_quant(0, 1)
+        mx1(0, 0)
+        mx1(0, 1)
+        w1_tile(1, yps, "y")
+        w1_tile(2, yps, "y")
+        w1_tile(3, tps, "t")
+        w1_quant(1)
+        w1_quant(2)
+        w1_quant(3)
+        mx1(1, 0)
+        gelu(0)
+        for bb in range(2):
+            pw2 = yps.tile([P, 1024], BF16, name="pw2_%d" % bb, tag="y")
+            for k in range(8):
+                nc.tensor.transpose(
+                    out=pw2[:, k * P:(k + 1) * P],
+                    in_=w2sb[:, bb * 1024 + k * P:bb * 1024 + (k + 1) * P],
+                    identity=identb[:],
+                )
+            nc.vector.tensor_copy(
+                out=w2g[:, bb * 1024:(bb + 1) * 1024].rearrange("p (b m t) -> p b m t", b=2, t=4),
+                in_=pw2[:].rearrange("p (b t m) -> p b m t", b=2, t=4),
+            )
+        nc.vector.quantize_mx(out=w2c[:].bitcast(FP8X4), scales=w2s[:], in_=w2g[:])
+
+        for j in range(10):
+            if j < 8:
+                tr(j)
+            if j + 1 < 8:
+                mx1(j + 1, 1)
+            if j == 0:
+                x_regroup(1, 0, 0, False)
+                x_regroup(1, 0, 1, False)
+                x_quant(1, 0)
+            if j == 1:
+                x_regroup(1, 1, 0, False)
+                x_regroup(1, 1, 1, False)
+                x_quant(1, 1)
+            if j + 2 < 8:
+                mx1(j + 2, 0)
+            if 1 <= j <= 8:
+                uevac(j - 1)
+            if j + 1 < 8:
+                gelu(j + 1)
+            if j >= 2:
+                yevac(j - 2)
+            if 1 <= j <= 8:
+                uquant(j - 1)
+                mx2(j - 1)

@@ -13,16 +13,36 @@ ALU = mybir.AluOpType
 
 P = 128
 FLOPS = 2 * 2 * 512 * 512 * 1024 * 2
-PIN = False
+PIN = True
 UEVAC_ON_VECTOR = ()
+ORDER = (
+    ("b2mm", 0, 0), ("w1T", 0, 0), ("b2ev", 0, 0), ("w1ev", 0, 0), ("xrS", 1, 0), ("xrV", 0, 0),
+    ("w1q", 0, 0), ("xrV", 0, 1), ("xrS", 1, 1), ("xq", 0, 0), ("b1f", 0, 0), ("w1T", 1, 0),
+    ("w1T", 2, 0), ("w1T", 3, 0), ("w1ev", 1, 0), ("mx1", 0, 0), ("w1q", 1, 0), ("xq", 1, 0),
+    ("g", 0, 0), ("w1ev", 2, 0), ("mx1", 0, 1), ("w1q", 2, 0), ("w1ev", 3, 0), ("mx1", 1, 0),
+    ("mx1", 1, 1), ("g", 0, 1), ("w1q", 3, 0), ("w2T", 0, 0), ("g", 1, 0), ("w2T", 1, 0),
+    ("w2ev", 0, 0), ("g", 1, 1), ("tr", 0, 0), ("mx1", 2, 0), ("uev", 0, 0), ("w2ev", 1, 0),
+    ("mx1", 2, 1), ("tr", 1, 0), ("mx1", 3, 0), ("g", 2, 0), ("w2q", 0, 0), ("g", 2, 1),
+    ("mx1", 3, 1), ("xrV", 2, 0), ("uev", 1, 0), ("xrV", 2, 1), ("tr", 2, 0), ("xq", 2, 0),
+    ("g", 3, 0), ("xrV", 3, 0), ("mx1", 4, 0), ("g", 3, 1), ("xrV", 3, 1), ("uev", 2, 0),
+    ("xq", 3, 0), ("uq", 0, 0), ("uq", 1, 0), ("mx1", 4, 1), ("g", 4, 0), ("mx2", 0, 0),
+    ("mx2", 0, 1), ("g", 4, 1), ("tr", 3, 0), ("yev", 0, 0), ("yev", 0, 1), ("mx2", 1, 0),
+    ("uev", 3, 0), ("mx2", 1, 1), ("uq", 2, 0), ("mx1", 5, 0), ("yev", 1, 0), ("mx1", 5, 1),
+    ("tr", 4, 0), ("g", 5, 0), ("yev", 1, 1), ("mx2", 2, 0), ("g", 5, 1), ("uq", 3, 0),
+    ("mx2", 2, 1), ("uev", 4, 0), ("mx1", 6, 0), ("yev", 2, 0), ("mx1", 6, 1), ("mx2", 3, 0),
+    ("yev", 2, 1), ("mx2", 3, 1), ("g", 6, 0), ("tr", 5, 0), ("yev", 3, 0), ("g", 6, 1),
+    ("mx1", 7, 0), ("yev", 3, 1), ("mx1", 7, 1), ("uev", 5, 0), ("uq", 4, 0), ("tr", 6, 0),
+    ("mx2", 4, 0), ("g", 7, 0), ("uq", 5, 0), ("mx2", 4, 1), ("yev", 4, 0), ("g", 7, 1),
+    ("mx2", 5, 0), ("yev", 4, 1), ("mx2", 5, 1), ("uev", 6, 0), ("tr", 7, 0), ("yev", 5, 0),
+    ("yev", 5, 1), ("uev", 7, 0), ("uq", 6, 0), ("mx2", 6, 0), ("uq", 7, 0), ("mx2", 6, 1),
+    ("yev", 6, 0), ("mx2", 7, 0), ("yev", 6, 1), ("mx2", 7, 1), ("yev", 7, 0), ("yev", 7, 1),
+)
 
 
 def tile_getspatialgatingweights_pa_kernel(tc, x_norm, w1_u, b1_u, w2, b2, out):
     nc = tc.nc
     with ExitStack() as ctx:
         const = ctx.enter_context(tc.tile_pool(name="const", bufs=1))
-        upool = ctx.enter_context(tc.tile_pool(name="upool", bufs=3))
-        opool = ctx.enter_context(tc.tile_pool(name="opool", bufs=4))
         zps = ctx.enter_context(tc.psum_pool(name="zps", bufs=3))
         tps = ctx.enter_context(tc.psum_pool(name="tps", bufs=2))
         yps = ctx.enter_context(tc.psum_pool(name="yps", bufs=3))
@@ -55,6 +75,11 @@ def tile_getspatialgatingweights_pa_kernel(tc, x_norm, w1_u, b1_u, w2, b2, out):
         xg = [const.tile([P, 2048], BF16, name="xg%d" % k, align_bytes=64) for k in range(4)]
         xc = [const.tile([P, 512], U32, name="xc%d" % k, align_bytes=64) for k in range(4)]
         xs = [const.tile([P, 512], U8, name="xs%d" % k, align_bytes=64) for k in range(4)]
+        usb = [const.tile([P, 1024], BF16, name="usb%d" % j) for j in range(8)]
+        ug = [const.tile([P, 1024], BF16, name="ug%d" % j, align_bytes=64) for j in range(8)]
+        uc = [const.tile([P, 256], U32, name="uc%d" % j, align_bytes=64) for j in range(8)]
+        us = [const.tile([P, 256], U8, name="us%d" % j, align_bytes=64) for j in range(8)]
+        osb = [const.tile([P, 1024], F32, name="osb%d" % j) for j in range(8)]
 
         nc.scalar.dma_start(out=b1bf[:], in_=b1_u.rearrange("(m a) -> m a", a=4))
         nc.gpsimd.memset(bz[:], 0.0)
@@ -73,68 +98,95 @@ def tile_getspatialgatingweights_pa_kernel(tc, x_norm, w1_u, b1_u, w2, b2, out):
                 out=xsb[1][:, 2 * u * 1024:(2 * u + 2) * 1024].rearrange("q (e v) -> q e v", e=2),
                 in_=xv[1, u],
             )
-
-        make_identity(nc, identf[:])
         nc.gpsimd.memset(ones[:], 1.0)
+        make_identity(nc, identf[:])
         make_identity(nc, identb[:])
         nc.vector.memset(warm[:], 0.0)
         nc.scalar.activation(out=warm2[:], in_=warm[:], func=ACT.Gelu)
-        nc.vector.tensor_copy(out=b1f[:], in_=b1bf[:])
 
         w1words = w1sb[:].bitcast(F32)
         w1gwords = w1g[:].bitcast(F32)
+        ps = {}
+        done = {}
 
-        def w1_tile(a, pool, tag):
-            pw = pool.tile([P, 256], F32, name="pw%d" % a, tag=tag)
+        def op_b1f(i, k):
+            nc.vector.tensor_copy(out=b1f[:], in_=b1bf[:])
+
+        def op_b2mm(i, k):
+            ps["pb"] = tps.tile([P, 512], F32, name="pb", tag="t")
+            nc.tensor.matmul(out=ps["pb"][:], lhsT=ones[:], rhs=bz[:], start=True, stop=True)
+
+        def op_b2ev(i, k):
+            nc.scalar.copy(out=b2bc[:], in_=ps["pb"][:])
+
+        def op_w1T(a, k):
+            if a == 3:
+                pw = tps.tile([P, 256], F32, name="pw%d" % a, tag="t")
+            else:
+                pw = yps.tile([P, 256], F32, name="pw%d" % a, tag="y")
+            ps[("pw", a)] = pw
             for u in range(2):
                 nc.tensor.transpose(
                     out=pw[:, u * P:(u + 1) * P],
                     in_=w1words[:, a * 256 + u * P:a * 256 + (u + 1) * P],
                     identity=identf[:],
                 )
+
+        def op_w1ev(a, k):
             nc.vector.tensor_copy(
                 out=w1gwords[:, a * 256:(a + 1) * 256].rearrange("q (m u) -> q m u", u=2),
-                in_=pw[:].rearrange("q (u m) -> q m u", u=2),
+                in_=ps[("pw", a)][:].rearrange("q (u m) -> q m u", u=2),
             )
 
-        def w1_quant(a):
+        def op_w1q(a, k):
             nc.vector.quantize_mx(
                 out=w1c[:, a * P:(a + 1) * P].bitcast(FP8X4),
                 scales=w1s[:, a * P:(a + 1) * P],
                 in_=w1g[:, a * 512:(a + 1) * 512],
             )
 
-        def x_regroup(n, ph, hf, on_scalar):
-            k = 2 * n + ph
+        def op_xrV(k, hf):
+            n, ph = k // 2, k % 2
             s0, s1 = hf * 32, (hf + 1) * 32
-            if on_scalar:
-                nc.scalar.copy(
-                    out=xg[k][:].rearrange("q (s i t) -> q s i t", i=8, t=4)[:, s0:s1],
-                    in_=xsb[n][:].rearrange("q (t s h i) -> q h s i t", t=4, h=2, i=8)[:, ph, s0:s1],
-                )
-            else:
-                nc.vector.tensor_copy(
-                    out=xg[k][:].rearrange("q (s i t) -> q s t i", i=8, t=4)[:, s0:s1],
-                    in_=xsb[n][:].rearrange("q (t s h i) -> q h s t i", t=4, h=2, i=8)[:, ph, s0:s1],
-                )
+            nc.vector.tensor_copy(
+                out=xg[k][:].rearrange("q (s i t) -> q s t i", i=8, t=4)[:, s0:s1],
+                in_=xsb[n][:].rearrange("q (t s h i) -> q h s t i", t=4, h=2, i=8)[:, ph, s0:s1],
+            )
 
-        def x_quant(n, ph):
-            k = 2 * n + ph
+        def op_xrS(k, hf):
+            n, ph = k // 2, k % 2
+            s0, s1 = hf * 32, (hf + 1) * 32
+            nc.scalar.copy(
+                out=xg[k][:].rearrange("q (s i t) -> q s i t", i=8, t=4)[:, s0:s1],
+                in_=xsb[n][:].rearrange("q (t s h i) -> q h s i t", t=4, h=2, i=8)[:, ph, s0:s1],
+            )
+
+        def op_xq(k, z):
             nc.vector.quantize_mx(out=xc[k][:].bitcast(FP8X4), scales=xs[k][:], in_=xg[k][:])
 
-        zt = {}
-        usb = {}
-        utp = {}
-        ugt = {}
-        uct = {}
-        ust = {}
-        yt = {}
-        osb = {}
+        def op_w2T(bb, z):
+            pw2 = yps.tile([P, 1024], BF16, name="pw2x%d" % bb, tag="y")
+            ps[("pw2", bb)] = pw2
+            for k in range(8):
+                nc.tensor.transpose(
+                    out=pw2[:, k * P:(k + 1) * P],
+                    in_=w2sb[:, bb * 1024 + k * P:bb * 1024 + (k + 1) * P],
+                    identity=identb[:],
+                )
 
-        def mx1(j, ph):
+        def op_w2ev(bb, z):
+            nc.vector.tensor_copy(
+                out=w2g[:, bb * 1024:(bb + 1) * 1024].rearrange("p (b m t) -> p b m t", b=2, t=4),
+                in_=ps[("pw2", bb)][:].rearrange("p (b t m) -> p b m t", b=2, t=4),
+            )
+
+        def op_w2q(i, k):
+            nc.vector.quantize_mx(out=w2c[:].bitcast(FP8X4), scales=w2s[:], in_=w2g[:])
+
+        def op_mx1(j, ph):
             n, a = j // 4, j % 4
-            z = zps.tile([P, 512], F32, name="z%d_%d" % (j, ph), tag="z")
-            zt[(j, ph)] = z
+            z = zps.tile([P, 512], F32, name="z%dx%d" % (j, ph), tag="z")
+            ps[("z", j, ph)] = z
             nc.tensor.matmul_mx(
                 out=z[:],
                 lhsT=w1c[:, a * P:(a + 1) * P].bitcast(FP8X4),
@@ -145,22 +197,19 @@ def tile_getspatialgatingweights_pa_kernel(tc, x_norm, w1_u, b1_u, w2, b2, out):
                 stop=True,
             )
 
-        def gelu(j):
+        def op_g(j, ph):
             a = j % 4
-            u_sb = upool.tile([P, 1024], BF16, name="usb%d" % j, tag="usb")
-            usb[j] = u_sb
-            for ph in range(2):
-                nc.scalar.activation(
-                    out=u_sb[:, ph * 512:(ph + 1) * 512],
-                    in_=zt[(j, ph)][:],
-                    func=ACT.Gelu,
-                    bias=b1f[:, a:a + 1],
-                    scale=1.0,
-                )
+            nc.scalar.activation(
+                out=usb[j][:, ph * 512:(ph + 1) * 512],
+                in_=ps[("z", j, ph)][:],
+                func=ACT.Gelu,
+                bias=b1f[:, a:a + 1],
+                scale=1.0,
+            )
 
-        def tr(j):
+        def op_tr(j, z):
             ut = tps.tile([P, 1024], BF16, name="ut%d" % j, tag="t")
-            utp[j] = ut
+            ps[("ut", j)] = ut
             for k in range(8):
                 nc.tensor.transpose(
                     out=ut[:, k * P:(k + 1) * P],
@@ -168,106 +217,45 @@ def tile_getspatialgatingweights_pa_kernel(tc, x_norm, w1_u, b1_u, w2, b2, out):
                     identity=identb[:],
                 )
 
-        def uevac(j):
-            ug = upool.tile([P, 1024], BF16, name="ug%d" % j, tag="ug", align_bytes=64)
-            ugt[j] = ug
-            dst = ug[:].rearrange("p (h m t) -> p h m t", h=2, t=4)
-            srcv = utp[j][:].rearrange("p (h t m) -> p h m t", h=2, t=4)
+        def op_uev(j, z):
+            dst = ug[j][:].rearrange("p (h m t) -> p h m t", h=2, t=4)
+            srcv = ps[("ut", j)][:].rearrange("p (h t m) -> p h m t", h=2, t=4)
             if j in UEVAC_ON_VECTOR:
                 nc.vector.tensor_copy(out=dst, in_=srcv)
             else:
                 nc.scalar.copy(out=dst, in_=srcv)
 
-        def uquant(j):
-            uc = upool.tile([P, 256], U32, name="uc%d" % j, tag="uc", align_bytes=64)
-            us = upool.tile([P, 256], U8, name="us%d" % j, tag="us", align_bytes=64)
-            uct[j] = uc
-            ust[j] = us
-            nc.vector.quantize_mx(out=uc[:].bitcast(FP8X4), scales=us[:], in_=ugt[j][:])
+        def op_uq(j, z):
+            nc.vector.quantize_mx(out=uc[j][:].bitcast(FP8X4), scales=us[j][:], in_=ug[j][:])
 
-        def mx2(j):
-            for ph in range(2):
-                y = yps.tile([P, 512], F32, name="y%d_%d" % (j, ph), tag="y")
-                yt[(j, ph)] = y
-                nc.tensor.matmul_mx(
-                    out=y[:],
-                    lhsT=uct[j][:, ph * P:(ph + 1) * P].bitcast(FP8X4),
-                    lhsT_scale=ust[j][:, ph * P:(ph + 1) * P],
-                    rhs=w2c[:].bitcast(FP8X4),
-                    rhs_scale=w2s[:],
-                    start=True,
-                    stop=True,
-                )
-
-        def yevac(j):
-            n, a = j // 4, j % 4
-            o_sb = opool.tile([P, 1024], F32, name="osb%d" % j, tag="osb")
-            osb[j] = o_sb
-            for ph in range(2):
-                nc.vector.tensor_tensor(
-                    out=o_sb[:].rearrange("m (s h i) -> m h s i", h=2, i=8)[:, ph],
-                    in0=yt[(j, ph)][:].rearrange("m (s i) -> m s i", i=8),
-                    in1=b2bc[:].rearrange("m (s i) -> m s i", i=8),
-                    op=ALU.add,
-                )
-            nc.sync.dma_start(out=ov[n, a], in_=o_sb[:])
-
-        w1_tile(0, yps, "y")
-        pb = tps.tile([P, 512], F32, name="pb", tag="t")
-        nc.tensor.matmul(out=pb[:], lhsT=ones[:], rhs=bz[:], start=True, stop=True)
-        nc.scalar.copy(out=b2bc[:], in_=pb[:])
-        x_regroup(0, 0, 0, False)
-        x_regroup(0, 1, 0, True)
-        w1_quant(0)
-        x_regroup(0, 0, 1, False)
-        x_regroup(0, 1, 1, True)
-        x_quant(0, 0)
-        x_quant(0, 1)
-        mx1(0, 0)
-        mx1(0, 1)
-        w1_tile(1, yps, "y")
-        w1_tile(2, yps, "y")
-        w1_tile(3, tps, "t")
-        w1_quant(1)
-        w1_quant(2)
-        w1_quant(3)
-        mx1(1, 0)
-        gelu(0)
-        for bb in range(2):
-            pw2 = yps.tile([P, 1024], BF16, name="pw2_%d" % bb, tag="y")
-            for k in range(8):
-                nc.tensor.transpose(
-                    out=pw2[:, k * P:(k + 1) * P],
-                    in_=w2sb[:, bb * 1024 + k * P:bb * 1024 + (k + 1) * P],
-                    identity=identb[:],
-                )
-            nc.vector.tensor_copy(
-                out=w2g[:, bb * 1024:(bb + 1) * 1024].rearrange("p (b m t) -> p b m t", b=2, t=4),
-                in_=pw2[:].rearrange("p (b t m) -> p b m t", b=2, t=4),
+        def op_mx2(j, ph):
+            y = yps.tile([P, 512], F32, name="y%dx%d" % (j, ph), tag="y")
+            ps[("y", j, ph)] = y
+            nc.tensor.matmul_mx(
+                out=y[:],
+                lhsT=uc[j][:, ph * P:(ph + 1) * P].bitcast(FP8X4),
+                lhsT_scale=us[j][:, ph * P:(ph + 1) * P],
+                rhs=w2c[:].bitcast(FP8X4),
+                rhs_scale=w2s[:],
+                start=True,
+                stop=True,
             )
-        nc.vector.quantize_mx(out=w2c[:].bitcast(FP8X4), scales=w2s[:], in_=w2g[:])
 
-        for j in range(10):
-            if j < 8:
-                tr(j)
-            if j + 1 < 8:
-                mx1(j + 1, 1)
-            if j == 0:
-                x_regroup(1, 0, 0, False)
-                x_regroup(1, 0, 1, False)
-                x_quant(1, 0)
-            if j == 1:
-                x_regroup(1, 1, 0, False)
-                x_regroup(1, 1, 1, False)
-                x_quant(1, 1)
-            if j + 2 < 8:
-                mx1(j + 2, 0)
-            if 1 <= j <= 8:
-                uevac(j - 1)
-            if j + 1 < 8:
-                gelu(j + 1)
-            if j >= 2:
-                yevac(j - 2)
-            if 1 <= j <= 8:
-                uquant(j - 1)
-                mx2(j - 1)
+        def op_yev(j, ph):
+            nc.vector.tensor_tensor(
+                out=osb[j][:].rearrange("m (s h i) -> m h s i", h=2, i=8)[:, ph],
+                in0=ps[("y", j, ph)][:].rearrange("m (s i) -> m s i", i=8),
+                in1=b2bc[:].rearrange("m (s i) -> m s i", i=8),
+                op=ALU.add,
+            )
+            done[j] = done.get(j, 0) + 1
+            if done[j] == 2:
+                nc.sync.dma_start(out=ov[j // 4, j % 4], in_=osb[j][:])
+
+        ops = {
+            "b1f": op_b1f, "b2mm": op_b2mm, "b2ev": op_b2ev, "w1T": op_w1T, "w1ev": op_w1ev, "w1q": op_w1q,
+            "xrV": op_xrV, "xrS": op_xrS, "xq": op_xq, "w2T": op_w2T, "w2ev": op_w2ev, "w2q": op_w2q,
+            "mx1": op_mx1, "g": op_g, "tr": op_tr, "uev": op_uev, "uq": op_uq, "mx2": op_mx2, "yev": op_yev,
+        }
+        for name, i, k in ORDER:
+            ops[name](i, k)

@@ -14,28 +14,33 @@ ALU = mybir.AluOpType
 P = 128
 FLOPS = 2 * 2 * 512 * 512 * 1024 * 2
 PIN = True
-UEVAC_ON_VECTOR = ()
 ORDER = (
-    ("b2mm", 0, 0), ("w1T", 0, 0), ("b2ev", 0, 0), ("w1ev", 0, 0), ("xrS", 1, 0), ("xrV", 0, 0),
-    ("w1q", 0, 0), ("xrV", 0, 1), ("xrS", 1, 1), ("xq", 0, 0), ("b1f", 0, 0), ("w1T", 1, 0),
-    ("w1T", 2, 0), ("w1T", 3, 0), ("w1ev", 1, 0), ("mx1", 0, 0), ("w1q", 1, 0), ("xq", 1, 0),
-    ("g", 0, 0), ("w1ev", 2, 0), ("mx1", 0, 1), ("w1q", 2, 0), ("w1ev", 3, 0), ("mx1", 1, 0),
-    ("mx1", 1, 1), ("g", 0, 1), ("w1q", 3, 0), ("w2T", 0, 0), ("g", 1, 0), ("w2T", 1, 0),
-    ("w2ev", 0, 0), ("g", 1, 1), ("tr", 0, 0), ("mx1", 2, 0), ("uev", 0, 0), ("w2ev", 1, 0),
-    ("mx1", 2, 1), ("tr", 1, 0), ("mx1", 3, 0), ("g", 2, 0), ("w2q", 0, 0), ("g", 2, 1),
-    ("mx1", 3, 1), ("xrV", 2, 0), ("uev", 1, 0), ("xrV", 2, 1), ("tr", 2, 0), ("xq", 2, 0),
-    ("g", 3, 0), ("xrV", 3, 0), ("mx1", 4, 0), ("g", 3, 1), ("xrV", 3, 1), ("uev", 2, 0),
-    ("xq", 3, 0), ("uq", 0, 0), ("uq", 1, 0), ("mx1", 4, 1), ("g", 4, 0), ("mx2", 0, 0),
-    ("mx2", 0, 1), ("g", 4, 1), ("tr", 3, 0), ("yev", 0, 0), ("yev", 0, 1), ("mx2", 1, 0),
-    ("uev", 3, 0), ("mx2", 1, 1), ("uq", 2, 0), ("mx1", 5, 0), ("yev", 1, 0), ("mx1", 5, 1),
-    ("tr", 4, 0), ("g", 5, 0), ("yev", 1, 1), ("mx2", 2, 0), ("g", 5, 1), ("uq", 3, 0),
-    ("mx2", 2, 1), ("uev", 4, 0), ("mx1", 6, 0), ("yev", 2, 0), ("mx1", 6, 1), ("mx2", 3, 0),
-    ("yev", 2, 1), ("mx2", 3, 1), ("g", 6, 0), ("tr", 5, 0), ("yev", 3, 0), ("g", 6, 1),
-    ("mx1", 7, 0), ("yev", 3, 1), ("mx1", 7, 1), ("uev", 5, 0), ("uq", 4, 0), ("tr", 6, 0),
-    ("mx2", 4, 0), ("g", 7, 0), ("uq", 5, 0), ("mx2", 4, 1), ("yev", 4, 0), ("g", 7, 1),
-    ("mx2", 5, 0), ("yev", 4, 1), ("mx2", 5, 1), ("uev", 6, 0), ("tr", 7, 0), ("yev", 5, 0),
-    ("yev", 5, 1), ("uev", 7, 0), ("uq", 6, 0), ("mx2", 6, 0), ("uq", 7, 0), ("mx2", 6, 1),
-    ("yev", 6, 0), ("mx2", 7, 0), ("yev", 6, 1), ("mx2", 7, 1), ("yev", 7, 0), ("yev", 7, 1),
+    ("b2mm", 0, 0, 0), ("w1T", 0, 0, 0), ("w1ev", 0, 0, 0), ("xe", 0, 0, 1), ("xe", 0, 1, 0),
+    ("xw", 0, 0, 0), ("b2ev", 0, 0, 0), ("w1q", 0, 0, 0), ("xq", 0, 0, 0), ("xe", 1, 0, 1),
+    ("b1f", 0, 0, 0), ("xw", 0, 1, 0), ("xe", 1, 1, 1), ("w1T", 1, 0, 0), ("w1T", 2, 0, 0),
+    ("w1T", 3, 0, 0), ("w1ev", 1, 0, 1), ("xq", 1, 0, 0), ("mx1", 0, 0, 0), ("w1q", 1, 0, 0),
+    ("w1ev", 2, 0, 0), ("g", 0, 0, 0), ("mx1", 0, 1, 0), ("w1ev", 3, 0, 0), ("mx1", 1, 0, 0),
+    ("w1q", 2, 0, 0), ("mx1", 1, 1, 0), ("g", 0, 1, 0), ("w1q", 3, 0, 0), ("w2T", 1, 0, 0),
+    ("g", 1, 0, 0), ("w2T", 0, 0, 0), ("w2ev", 1, 0, 0), ("tr", 0, 0, 0), ("g", 1, 1, 0),
+    ("w2ev", 0, 0, 0), ("mx1", 2, 0, 0), ("uev", 0, 0, 1), ("mx1", 2, 1, 0), ("xw", 3, 1, 0),
+    ("mx1", 3, 0, 0), ("tr", 1, 0, 0), ("xw", 3, 0, 0), ("g", 2, 0, 0), ("xw", 2, 0, 0),
+    ("g", 3, 0, 0), ("mx1", 3, 1, 0), ("xq", 3, 0, 0), ("g", 2, 1, 0), ("xw", 2, 1, 0),
+    ("uev", 1, 0, 1), ("tr", 2, 0, 0), ("uq", 0, 0, 0), ("xq", 2, 0, 0), ("mx1", 4, 1, 0),
+    ("g", 3, 1, 0), ("w2q", 0, 0, 0), ("mx1", 4, 0, 0), ("uq", 1, 0, 0), ("g", 4, 1, 0),
+    ("tr", 3, 0, 0), ("uev", 2, 0, 0), ("g", 4, 0, 0), ("mx2", 0, 0, 0), ("mx2", 0, 1, 0),
+    ("uev", 3, 0, 1), ("mx1", 5, 1, 0), ("yev", 0, 0, 0), ("mx2", 1, 0, 0), ("mx1", 5, 0, 0),
+    ("uq", 2, 0, 0), ("mx1", 6, 1, 0), ("yev", 0, 1, 0), ("g", 5, 1, 0), ("mx2", 1, 1, 0),
+    ("tr", 4, 0, 0), ("uq", 3, 0, 0), ("g", 6, 1, 0), ("yev", 1, 0, 0), ("mx2", 2, 0, 0),
+    ("g", 5, 0, 0), ("yev", 1, 1, 0), ("mx2", 2, 1, 0), ("mx1", 6, 0, 0), ("uev", 4, 0, 1),
+    ("yev", 2, 0, 0), ("mx2", 3, 0, 0), ("tr", 5, 0, 0), ("yev", 2, 1, 0), ("g", 6, 0, 0),
+    ("mx2", 3, 1, 0), ("uq", 4, 0, 0), ("uev", 5, 0, 1), ("yev", 3, 0, 0), ("tr", 6, 0, 0),
+    ("yev", 3, 1, 0), ("mx2", 4, 0, 0), ("uev", 6, 0, 1), ("mx2", 4, 1, 0), ("uq", 5, 0, 0),
+    ("mx1", 7, 0, 0), ("yev", 4, 0, 0), ("mx1", 7, 1, 0), ("mx2", 5, 0, 0), ("yev", 4, 1, 0),
+    ("g", 7, 0, 0), ("mx2", 5, 1, 0), ("uq", 6, 0, 0), ("g", 7, 1, 0), ("trh", 7, 0, 0),
+    ("yev", 5, 0, 0), ("mx2", 6, 1, 0), ("uevh", 7, 0, 1), ("yev", 5, 1, 0), ("trh", 7, 1, 0),
+    ("mx2", 6, 0, 0), ("yev", 6, 1, 0), ("uevh", 7, 1, 1), ("uqh", 7, 0, 0), ("yev", 6, 0, 0),
+    ("mx2", 7, 0, 0), ("uqh", 7, 1, 0), ("yevh", 0, 0, 0), ("mx2", 7, 1, 0), ("yevh", 0, 1, 0),
+    ("yevh", 1, 0, 0), ("yevh", 1, 1, 0),
 )
 
 
@@ -106,20 +111,28 @@ def tile_getspatialgatingweights_pa_kernel(tc, x_norm, w1_u, b1_u, w2, b2, out):
 
         w1words = w1sb[:].bitcast(F32)
         w1gwords = w1g[:].bitcast(F32)
+        w2words = w2sb[:].bitcast(F32)
+        w2gwords = w2g[:].bitcast(F32)
         ps = {}
         done = {}
 
-        def op_b1f(i, k):
+        def copy_on(eng, dst, srcv):
+            if eng == 1:
+                nc.scalar.copy(out=dst, in_=srcv)
+            else:
+                nc.vector.tensor_copy(out=dst, in_=srcv)
+
+        def op_b1f(i, k, eng):
             nc.vector.tensor_copy(out=b1f[:], in_=b1bf[:])
 
-        def op_b2mm(i, k):
+        def op_b2mm(i, k, eng):
             ps["pb"] = tps.tile([P, 512], F32, name="pb", tag="t")
             nc.tensor.matmul(out=ps["pb"][:], lhsT=ones[:], rhs=bz[:], start=True, stop=True)
 
-        def op_b2ev(i, k):
+        def op_b2ev(i, k, eng):
             nc.scalar.copy(out=b2bc[:], in_=ps["pb"][:])
 
-        def op_w1T(a, k):
+        def op_w1T(a, k, eng):
             if a == 3:
                 pw = tps.tile([P, 256], F32, name="pw%d" % a, tag="t")
             else:
@@ -132,103 +145,129 @@ def tile_getspatialgatingweights_pa_kernel(tc, x_norm, w1_u, b1_u, w2, b2, out):
                     identity=identf[:],
                 )
 
-        def op_w1ev(a, k):
-            nc.vector.tensor_copy(
-                out=w1gwords[:, a * 256:(a + 1) * 256].rearrange("q (m u) -> q m u", u=2),
-                in_=ps[("pw", a)][:].rearrange("q (u m) -> q m u", u=2),
+        def op_w1ev(a, k, eng):
+            copy_on(
+                eng,
+                w1gwords[:, a * 256:(a + 1) * 256].rearrange("q (m u) -> q m u", u=2),
+                ps[("pw", a)][:].rearrange("q (u m) -> q m u", u=2),
             )
 
-        def op_w1q(a, k):
+        def op_w1q(a, k, eng):
             nc.vector.quantize_mx(
                 out=w1c[:, a * P:(a + 1) * P].bitcast(FP8X4),
                 scales=w1s[:, a * P:(a + 1) * P],
                 in_=w1g[:, a * 512:(a + 1) * 512],
             )
 
-        def op_xrV(k, hf):
-            n, ph = k // 2, k % 2
-            s0, s1 = hf * 32, (hf + 1) * 32
+        def op_xw(key, hf, eng):
+            n, ph = key // 2, key % 2
+            if n == 0:
+                dst = xg[hf][:, ph * 1024:(ph + 1) * 1024]
+            else:
+                dst = xg[2 + ph][:, hf * 1024:(hf + 1) * 1024]
             nc.vector.tensor_copy(
-                out=xg[k][:].rearrange("q (s i t) -> q s t i", i=8, t=4)[:, s0:s1],
-                in_=xsb[n][:].rearrange("q (t s h i) -> q h s t i", t=4, h=2, i=8)[:, ph, s0:s1],
+                out=dst.rearrange("q (e s i t) -> q s t i e", e=2, s=32, i=4),
+                in_=xsb[n][:].rearrange("q (t s h i e) -> q h s t i e", t=4, h=2, i=4, e=2)[:, ph, hf * 32:(hf + 1) * 32],
             )
 
-        def op_xrS(k, hf):
-            n, ph = k // 2, k % 2
-            s0, s1 = hf * 32, (hf + 1) * 32
-            nc.scalar.copy(
-                out=xg[k][:].rearrange("q (s i t) -> q s i t", i=8, t=4)[:, s0:s1],
-                in_=xsb[n][:].rearrange("q (t s h i) -> q h s i t", t=4, h=2, i=8)[:, ph, s0:s1],
+        def op_xe(hf, e, eng):
+            copy_on(
+                eng,
+                xg[hf][:, 1024 + e * 512:1024 + (e + 1) * 512].rearrange("q (s i t) -> q s i t", s=32, i=4),
+                xsb[0][:].rearrange("q (t s h i e) -> q h e s i t", t=4, h=2, i=4, e=2)[:, 1, e, hf * 32:(hf + 1) * 32],
             )
 
-        def op_xq(k, z):
+        def op_xq(k, z, eng):
             nc.vector.quantize_mx(out=xc[k][:].bitcast(FP8X4), scales=xs[k][:], in_=xg[k][:])
 
-        def op_w2T(bb, z):
-            pw2 = yps.tile([P, 1024], BF16, name="pw2x%d" % bb, tag="y")
+        def op_w2T(bb, z, eng):
+            pw2 = yps.tile([P, 512], F32, name="pw2x%d" % bb, tag="y")
             ps[("pw2", bb)] = pw2
-            for k in range(8):
+            for k in range(4):
                 nc.tensor.transpose(
                     out=pw2[:, k * P:(k + 1) * P],
-                    in_=w2sb[:, bb * 1024 + k * P:bb * 1024 + (k + 1) * P],
-                    identity=identb[:],
+                    in_=w2words[:, bb * 512 + k * P:bb * 512 + (k + 1) * P],
+                    identity=identf[:],
                 )
 
-        def op_w2ev(bb, z):
-            nc.vector.tensor_copy(
-                out=w2g[:, bb * 1024:(bb + 1) * 1024].rearrange("p (b m t) -> p b m t", b=2, t=4),
-                in_=ps[("pw2", bb)][:].rearrange("p (b t m) -> p b m t", b=2, t=4),
+        def op_w2ev(bb, z, eng):
+            copy_on(
+                eng,
+                w2gwords[:, bb * 512:(bb + 1) * 512].rearrange("q (b m u) -> q b m u", b=2, u=2),
+                ps[("pw2", bb)][:].rearrange("q (b u m) -> q b m u", b=2, u=2),
             )
 
-        def op_w2q(i, k):
+        def op_w2q(i, k, eng):
             nc.vector.quantize_mx(out=w2c[:].bitcast(FP8X4), scales=w2s[:], in_=w2g[:])
 
-        def op_mx1(j, ph):
+        def op_mx1(j, x, eng):
             n, a = j // 4, j % 4
-            z = zps.tile([P, 512], F32, name="z%dx%d" % (j, ph), tag="z")
-            ps[("z", j, ph)] = z
+            z = zps.tile([P, 512], F32, name="z%dx%d" % (j, x), tag="z")
+            ps[("z", j, x)] = z
             nc.tensor.matmul_mx(
                 out=z[:],
                 lhsT=w1c[:, a * P:(a + 1) * P].bitcast(FP8X4),
                 lhsT_scale=w1s[:, a * P:(a + 1) * P],
-                rhs=xc[2 * n + ph][:].bitcast(FP8X4),
-                rhs_scale=xs[2 * n + ph][:],
+                rhs=xc[2 * n + x][:].bitcast(FP8X4),
+                rhs_scale=xs[2 * n + x][:],
                 start=True,
                 stop=True,
             )
 
-        def op_g(j, ph):
+        def op_g(j, x, eng):
             a = j % 4
             nc.scalar.activation(
-                out=usb[j][:, ph * 512:(ph + 1) * 512],
-                in_=ps[("z", j, ph)][:],
+                out=usb[j][:, x * 512:(x + 1) * 512],
+                in_=ps[("z", j, x)][:],
                 func=ACT.Gelu,
                 bias=b1f[:, a:a + 1],
                 scale=1.0,
             )
 
-        def op_tr(j, z):
+        def u_block(j, ph, t):
+            if j < 4:
+                return (t // 2) * 512 + ph * 256 + (t % 2) * P
+            return ph * 512 + t * P
+
+        def op_tr(j, z, eng):
             ut = tps.tile([P, 1024], BF16, name="ut%d" % j, tag="t")
             ps[("ut", j)] = ut
             for k in range(8):
-                nc.tensor.transpose(
-                    out=ut[:, k * P:(k + 1) * P],
-                    in_=usb[j][:, k * P:(k + 1) * P],
-                    identity=identb[:],
-                )
+                c0 = u_block(j, k // 4, k % 4)
+                nc.tensor.transpose(out=ut[:, k * P:(k + 1) * P], in_=usb[j][:, c0:c0 + P], identity=identb[:])
 
-        def op_uev(j, z):
-            dst = ug[j][:].rearrange("p (h m t) -> p h m t", h=2, t=4)
-            srcv = ps[("ut", j)][:].rearrange("p (h t m) -> p h m t", h=2, t=4)
-            if j in UEVAC_ON_VECTOR:
-                nc.vector.tensor_copy(out=dst, in_=srcv)
-            else:
-                nc.scalar.copy(out=dst, in_=srcv)
+        def op_trh(j, ph, eng):
+            ut = tps.tile([P, 512], BF16, name="ut%dx%d" % (j, ph), tag="t")
+            ps[("uth", j, ph)] = ut
+            for t in range(4):
+                c0 = u_block(j, ph, t)
+                nc.tensor.transpose(out=ut[:, t * P:(t + 1) * P], in_=usb[j][:, c0:c0 + P], identity=identb[:])
 
-        def op_uq(j, z):
+        def op_uev(j, z, eng):
+            copy_on(
+                eng,
+                ug[j][:].rearrange("p (h m t) -> p h m t", h=2, t=4),
+                ps[("ut", j)][:].rearrange("p (h t m) -> p h m t", h=2, t=4),
+            )
+
+        def op_uevh(j, ph, eng):
+            copy_on(
+                eng,
+                ug[j][:, ph * 512:(ph + 1) * 512].rearrange("p (m t) -> p m t", t=4),
+                ps[("uth", j, ph)][:].rearrange("p (t m) -> p m t", t=4),
+            )
+
+        def op_uq(j, z, eng):
             nc.vector.quantize_mx(out=uc[j][:].bitcast(FP8X4), scales=us[j][:], in_=ug[j][:])
 
-        def op_mx2(j, ph):
+        def op_uqh(j, ph, eng):
+            nc.vector.quantize_mx(
+                out=uc[j][:, ph * P:(ph + 1) * P].bitcast(FP8X4),
+                scales=us[j][:, ph * P:(ph + 1) * P],
+                in_=ug[j][:, ph * 512:(ph + 1) * 512],
+            )
+
+        def op_mx2(j, ph, eng):
             y = yps.tile([P, 512], F32, name="y%dx%d" % (j, ph), tag="y")
             ps[("y", j, ph)] = y
             nc.tensor.matmul_mx(
@@ -241,21 +280,31 @@ def tile_getspatialgatingweights_pa_kernel(tc, x_norm, w1_u, b1_u, w2, b2, out):
                 stop=True,
             )
 
-        def op_yev(j, ph):
+        def y_add(j, ph, s0, s1):
             nc.vector.tensor_tensor(
-                out=osb[j][:].rearrange("m (s h i) -> m h s i", h=2, i=8)[:, ph],
-                in0=ps[("y", j, ph)][:].rearrange("m (s i) -> m s i", i=8),
-                in1=b2bc[:].rearrange("m (s i) -> m s i", i=8),
+                out=osb[j][:].rearrange("m (s h i) -> m h s i", h=2, i=8)[:, ph, s0:s1],
+                in0=ps[("y", j, ph)][:].rearrange("m (s i) -> m s i", i=8)[:, s0:s1],
+                in1=b2bc[:].rearrange("m (s i) -> m s i", i=8)[:, s0:s1],
                 op=ALU.add,
             )
+
+        def op_yev(j, ph, eng):
+            y_add(j, ph, 0, 64)
             done[j] = done.get(j, 0) + 1
             if done[j] == 2:
                 nc.sync.dma_start(out=ov[j // 4, j % 4], in_=osb[j][:])
 
+        def op_yevh(ph, half, eng):
+            y_add(7, ph, half * 32, (half + 1) * 32)
+            done[(7, half)] = done.get((7, half), 0) + 1
+            if done[(7, half)] == 2:
+                nc.sync.dma_start(out=ov[1, 3][:, half * 512:(half + 1) * 512], in_=osb[7][:, half * 512:(half + 1) * 512])
+
         ops = {
             "b1f": op_b1f, "b2mm": op_b2mm, "b2ev": op_b2ev, "w1T": op_w1T, "w1ev": op_w1ev, "w1q": op_w1q,
-            "xrV": op_xrV, "xrS": op_xrS, "xq": op_xq, "w2T": op_w2T, "w2ev": op_w2ev, "w2q": op_w2q,
-            "mx1": op_mx1, "g": op_g, "tr": op_tr, "uev": op_uev, "uq": op_uq, "mx2": op_mx2, "yev": op_yev,
+            "xw": op_xw, "xe": op_xe, "xq": op_xq, "w2T": op_w2T, "w2ev": op_w2ev, "w2q": op_w2q,
+            "mx1": op_mx1, "g": op_g, "tr": op_tr, "trh": op_trh, "uev": op_uev, "uevh": op_uevh,
+            "uq": op_uq, "uqh": op_uqh, "mx2": op_mx2, "yev": op_yev, "yevh": op_yevh,
         }
-        for name, i, k in ORDER:
-            ops[name](i, k)
+        for name, i, k, eng in ORDER:
+            ops[name](i, k, eng)

@@ -60,7 +60,6 @@ def tile_getspatialgatingweights_pa_kernel(tc, x_norm, w1_u, b1_u, w2, b2, out):
         ov = out.rearrange("n (m a) d h w -> n a m (d h w)", a=4)
 
         identf = const.tile([P, P], F32, name="identf")
-        identb = const.tile([P, P], BF16, name="identb")
         ones = const.tile([P, P], BF16, name="ones")
         bz = const.tile([P, 512], BF16, name="bz")
         b2bc = const.tile([P, 512], F32, name="b2bc")
@@ -105,7 +104,6 @@ def tile_getspatialgatingweights_pa_kernel(tc, x_norm, w1_u, b1_u, w2, b2, out):
             )
         nc.gpsimd.memset(ones[:], 1.0)
         make_identity(nc, identf[:])
-        make_identity(nc, identb[:])
         nc.vector.memset(warm[:], 0.0)
         nc.scalar.activation(out=warm2[:], in_=warm[:], func=ACT.Gelu)
 
@@ -166,15 +164,15 @@ def tile_getspatialgatingweights_pa_kernel(tc, x_norm, w1_u, b1_u, w2, b2, out):
             else:
                 dst = xg[2 + ph][:, hf * 1024:(hf + 1) * 1024]
             nc.vector.tensor_copy(
-                out=dst.rearrange("q (e s i t) -> q s t i e", e=2, s=32, i=4),
-                in_=xsb[n][:].rearrange("q (t s h i e) -> q h s t i e", t=4, h=2, i=4, e=2)[:, ph, hf * 32:(hf + 1) * 32],
+                out=dst.rearrange("q (s i t) -> q s t i", s=32, i=8),
+                in_=xsb[n][:].rearrange("q (t s h i) -> q h s t i", t=4, h=2, i=8)[:, ph, hf * 32:(hf + 1) * 32],
             )
 
         def op_xe(hf, e, eng):
             copy_on(
                 eng,
-                xg[hf][:, 1024 + e * 512:1024 + (e + 1) * 512].rearrange("q (s i t) -> q s i t", s=32, i=4),
-                xsb[0][:].rearrange("q (t s h i e) -> q h e s i t", t=4, h=2, i=4, e=2)[:, 1, e, hf * 32:(hf + 1) * 32],
+                xg[hf][:, 1024 + e * 512:1024 + (e + 1) * 512].rearrange("q (s i t) -> q s t i", s=16, i=8),
+                xsb[0][:].rearrange("q (t s h i) -> q h s t i", t=4, h=2, i=8)[:, 1, hf * 32 + e * 16:hf * 32 + (e + 1) * 16],
             )
 
         def op_xq(k, z, eng):
@@ -224,37 +222,34 @@ def tile_getspatialgatingweights_pa_kernel(tc, x_norm, w1_u, b1_u, w2, b2, out):
                 scale=1.0,
             )
 
-        def u_block(j, ph, t):
-            if j < 4:
-                return (t // 2) * 512 + ph * 256 + (t % 2) * P
-            return ph * 512 + t * P
+        def u_words(j, ph, u):
+            w0 = u * 256 + ph * P if j < 4 else ph * 256 + u * P
+            return usb[j][:].bitcast(F32)[:, w0:w0 + P]
 
         def op_tr(j, z, eng):
-            ut = tps.tile([P, 1024], BF16, name="ut%d" % j, tag="t")
+            ut = tps.tile([P, 512], F32, name="ut%d" % j, tag="t")
             ps[("ut", j)] = ut
-            for k in range(8):
-                c0 = u_block(j, k // 4, k % 4)
-                nc.tensor.transpose(out=ut[:, k * P:(k + 1) * P], in_=usb[j][:, c0:c0 + P], identity=identb[:])
+            for k in range(4):
+                nc.tensor.transpose(out=ut[:, k * P:(k + 1) * P], in_=u_words(j, k // 2, k % 2), identity=identf[:])
 
         def op_trh(j, ph, eng):
-            ut = tps.tile([P, 512], BF16, name="ut%dx%d" % (j, ph), tag="t")
+            ut = tps.tile([P, 256], F32, name="ut%dx%d" % (j, ph), tag="t")
             ps[("uth", j, ph)] = ut
-            for t in range(4):
-                c0 = u_block(j, ph, t)
-                nc.tensor.transpose(out=ut[:, t * P:(t + 1) * P], in_=usb[j][:, c0:c0 + P], identity=identb[:])
+            for u in range(2):
+                nc.tensor.transpose(out=ut[:, u * P:(u + 1) * P], in_=u_words(j, ph, u), identity=identf[:])
 
         def op_uev(j, z, eng):
             copy_on(
                 eng,
-                ug[j][:].rearrange("p (h m t) -> p h m t", h=2, t=4),
-                ps[("ut", j)][:].rearrange("p (h t m) -> p h m t", h=2, t=4),
+                ug[j][:].bitcast(F32).rearrange("p (h m u) -> p h m u", h=2, u=2),
+                ps[("ut", j)][:].rearrange("p (h u m) -> p h m u", h=2, u=2),
             )
 
         def op_uevh(j, ph, eng):
             copy_on(
                 eng,
-                ug[j][:, ph * 512:(ph + 1) * 512].rearrange("p (m t) -> p m t", t=4),
-                ps[("uth", j, ph)][:].rearrange("p (t m) -> p m t", t=4),
+                ug[j][:].bitcast(F32)[:, ph * 256:(ph + 1) * 256].rearrange("p (m u) -> p m u", u=2),
+                ps[("uth", j, ph)][:].rearrange("p (u m) -> p m u", u=2),
             )
 
         def op_uq(j, z, eng):

@@ -13,48 +13,19 @@ ALU = mybir.AluOpType
 
 P = 128
 FLOPS = 2 * 2 * 512 * 512 * 1024 * 2
-PIN = True
-ORDER = (
-    ("b2mm", 0, 0, 0), ("w1T", 0, 0, 0), ("w1ev", 0, 0, 0), ("xe", 0, 0, 1), ("xe", 0, 1, 0),
-    ("xw", 0, 0, 0), ("b2ev", 0, 0, 0), ("w1q", 0, 0, 0), ("xq", 0, 0, 0), ("xe", 1, 0, 1),
-    ("b1f", 0, 0, 0), ("xw", 0, 1, 0), ("xe", 1, 1, 1), ("w1T", 1, 0, 0), ("w1T", 2, 0, 0),
-    ("w1T", 3, 0, 0), ("w1ev", 1, 0, 1), ("xq", 1, 0, 0), ("mx1", 0, 0, 0), ("w1q", 1, 0, 0),
-    ("w1ev", 2, 0, 0), ("g", 0, 0, 0), ("mx1", 0, 1, 0), ("w1ev", 3, 0, 0), ("mx1", 1, 0, 0),
-    ("w1q", 2, 0, 0), ("mx1", 1, 1, 0), ("g", 0, 1, 0), ("w1q", 3, 0, 0), ("w2T", 1, 0, 0),
-    ("g", 1, 0, 0), ("w2T", 0, 0, 0), ("w2ev", 1, 0, 0), ("tr", 0, 0, 0), ("g", 1, 1, 0),
-    ("w2ev", 0, 0, 0), ("mx1", 2, 0, 0), ("uev", 0, 0, 1), ("mx1", 2, 1, 0), ("xw", 3, 1, 0),
-    ("mx1", 3, 0, 0), ("tr", 1, 0, 0), ("xw", 3, 0, 0), ("g", 2, 0, 0), ("xw", 2, 0, 0),
-    ("g", 3, 0, 0), ("mx1", 3, 1, 0), ("xq", 3, 0, 0), ("g", 2, 1, 0), ("xw", 2, 1, 0),
-    ("uev", 1, 0, 1), ("tr", 2, 0, 0), ("uq", 0, 0, 0), ("xq", 2, 0, 0), ("mx1", 4, 1, 0),
-    ("g", 3, 1, 0), ("w2q", 0, 0, 0), ("mx1", 4, 0, 0), ("uq", 1, 0, 0), ("g", 4, 1, 0),
-    ("tr", 3, 0, 0), ("uev", 2, 0, 0), ("g", 4, 0, 0), ("mx2", 0, 0, 0), ("mx2", 0, 1, 0),
-    ("uev", 3, 0, 1), ("mx1", 5, 1, 0), ("yev", 0, 0, 0), ("mx2", 1, 0, 0), ("mx1", 5, 0, 0),
-    ("uq", 2, 0, 0), ("mx1", 6, 1, 0), ("yev", 0, 1, 0), ("g", 5, 1, 0), ("mx2", 1, 1, 0),
-    ("tr", 4, 0, 0), ("uq", 3, 0, 0), ("g", 6, 1, 0), ("yev", 1, 0, 0), ("mx2", 2, 0, 0),
-    ("g", 5, 0, 0), ("yev", 1, 1, 0), ("mx2", 2, 1, 0), ("mx1", 6, 0, 0), ("uev", 4, 0, 1),
-    ("yev", 2, 0, 0), ("mx2", 3, 0, 0), ("tr", 5, 0, 0), ("yev", 2, 1, 0), ("g", 6, 0, 0),
-    ("mx2", 3, 1, 0), ("uq", 4, 0, 0), ("uev", 5, 0, 1), ("yev", 3, 0, 0), ("tr", 6, 0, 0),
-    ("yev", 3, 1, 0), ("mx2", 4, 0, 0), ("uev", 6, 0, 1), ("mx2", 4, 1, 0), ("uq", 5, 0, 0),
-    ("mx1", 7, 0, 0), ("yev", 4, 0, 0), ("mx1", 7, 1, 0), ("mx2", 5, 0, 0), ("yev", 4, 1, 0),
-    ("g", 7, 0, 0), ("mx2", 5, 1, 0), ("uq", 6, 0, 0), ("g", 7, 1, 0), ("trh", 7, 0, 0),
-    ("yev", 5, 0, 0), ("mx2", 6, 1, 0), ("uevh", 7, 0, 1), ("yev", 5, 1, 0), ("trh", 7, 1, 0),
-    ("mx2", 6, 0, 0), ("yev", 6, 1, 0), ("uevh", 7, 1, 1), ("uqh", 7, 0, 0), ("yev", 6, 0, 0),
-    ("mx2", 7, 0, 0), ("uqh", 7, 1, 0), ("yevh", 0, 0, 0), ("mx2", 7, 1, 0), ("yevh", 0, 1, 0),
-    ("yevh", 1, 0, 0), ("yevh", 1, 1, 0),
-)
+SLABS = 8
 
 
 def tile_getspatialgatingweights_pa_kernel(tc, x_norm, w1_u, b1_u, w2, b2, out):
     nc = tc.nc
     with ExitStack() as ctx:
         const = ctx.enter_context(tc.tile_pool(name="const", bufs=1))
-        zps = ctx.enter_context(tc.psum_pool(name="zps", bufs=3))
+        zps = ctx.enter_context(tc.psum_pool(name="zps", bufs=2))
         tps = ctx.enter_context(tc.psum_pool(name="tps", bufs=2))
-        yps = ctx.enter_context(tc.psum_pool(name="yps", bufs=3))
-        if PIN:
-            ctx.enter_context(tc.manual_schedule())
+        yps = ctx.enter_context(tc.psum_pool(name="yps", bufs=4))
+        ctx.enter_context(tc.manual_schedule())
 
-        xv = x_norm.rearrange("n (u q e) d h w -> n u q e (d h w)", u=2, e=2)
+        xv = x_norm.rearrange("n (q t) d h w -> n q t (d h w)", t=4)
         w1v = w1_u.rearrange("(m a) c -> m a c", a=4)
         w2v = w2.rearrange("(b m) g -> m b g", m=P)
         ov = out.rearrange("n (m a) d h w -> n a m (d h w)", a=4)
@@ -79,29 +50,26 @@ def tile_getspatialgatingweights_pa_kernel(tc, x_norm, w1_u, b1_u, w2, b2, out):
         xg = [const.tile([P, 2048], BF16, name="xg%d" % k, align_bytes=64) for k in range(4)]
         xc = [const.tile([P, 512], U32, name="xc%d" % k, align_bytes=64) for k in range(4)]
         xs = [const.tile([P, 512], U8, name="xs%d" % k, align_bytes=64) for k in range(4)]
-        usb = [const.tile([P, 1024], BF16, name="usb%d" % j) for j in range(8)]
-        ug = [const.tile([P, 1024], BF16, name="ug%d" % j, align_bytes=64) for j in range(8)]
-        uc = [const.tile([P, 256], U32, name="uc%d" % j, align_bytes=64) for j in range(8)]
-        us = [const.tile([P, 256], U8, name="us%d" % j, align_bytes=64) for j in range(8)]
-        osb = [const.tile([P, 1024], F32, name="osb%d" % j) for j in range(8)]
+        usb = [const.tile([P, 1024], BF16, name="usb%d" % j) for j in range(SLABS)]
+        ug = [const.tile([P, 1024], BF16, name="ug%d" % j, align_bytes=64) for j in range(SLABS)]
+        uc = [const.tile([P, 256], U32, name="uc%d" % j, align_bytes=64) for j in range(SLABS)]
+        us = [const.tile([P, 256], U8, name="us%d" % j, align_bytes=64) for j in range(SLABS)]
+        osb = [const.tile([P, 1024], F32, name="osb%d" % j) for j in range(SLABS)]
 
+        def load_x(n, v0, v1):
+            nc.sync.dma_start(out=xsb[n][:].rearrange("q (t v) -> q t v", t=4)[:, :, v0:v1], in_=xv[n][:, :, v0:v1])
+
+        nc.scalar.dma_start(out=w1sb[:, 0:512], in_=w1v[:, 0, :])
         nc.scalar.dma_start(out=b1bf[:], in_=b1_u.rearrange("(m a) -> m a", a=4))
         nc.gpsimd.memset(bz[:], 0.0)
         nc.scalar.dma_start(out=bz[0:1, :], in_=b2.rearrange("(o k) -> o k", o=1))
-        nc.sync.dma_start(out=w1sb[:, 0:512], in_=w1v[:, 0, :])
-        for hf in range(2):
-            for u in range(2):
-                nc.sync.dma_start(
-                    out=xsb[0][:].rearrange("q (t v) -> q t v", t=4)[:, 2 * u:2 * u + 2, hf * 512:(hf + 1) * 512],
-                    in_=xv[0, u][:, :, hf * 512:(hf + 1) * 512],
-                )
+        load_x(0, 0, 256)
+        load_x(0, 256, 512)
+        load_x(0, 512, 1024)
         nc.sync.dma_start(out=w1sb[:, 512:2048].rearrange("m (a c) -> m a c", a=3), in_=w1v[:, 1:4, :])
         nc.sync.dma_start(out=w2sb[:].rearrange("m (b g) -> m b g", b=4), in_=w2v)
-        for u in range(2):
-            nc.sync.dma_start(
-                out=xsb[1][:, 2 * u * 1024:(2 * u + 2) * 1024].rearrange("q (e v) -> q e v", e=2),
-                in_=xv[1, u],
-            )
+        load_x(1, 0, 512)
+        load_x(1, 512, 1024)
         nc.gpsimd.memset(ones[:], 1.0)
         make_identity(nc, identf[:])
         nc.vector.memset(warm[:], 0.0)
@@ -112,73 +80,62 @@ def tile_getspatialgatingweights_pa_kernel(tc, x_norm, w1_u, b1_u, w2, b2, out):
         w2words = w2sb[:].bitcast(F32)
         w2gwords = w2g[:].bitcast(F32)
         ps = {}
-        done = {}
 
         def copy_on(eng, dst, srcv):
-            if eng == 1:
+            if eng == "S":
                 nc.scalar.copy(out=dst, in_=srcv)
             else:
                 nc.vector.tensor_copy(out=dst, in_=srcv)
 
-        def op_b1f(i, k, eng):
-            nc.vector.tensor_copy(out=b1f[:], in_=b1bf[:])
+        def b2_spread():
+            pb = yps.tile([P, 512], F32, name="pb", tag="y")
+            ps["pb"] = pb
+            nc.tensor.matmul(out=pb[:], lhsT=ones[:], rhs=bz[:], start=True, stop=True)
 
-        def op_b2mm(i, k, eng):
-            ps["pb"] = tps.tile([P, 512], F32, name="pb", tag="t")
-            nc.tensor.matmul(out=ps["pb"][:], lhsT=ones[:], rhs=bz[:], start=True, stop=True)
-
-        def op_b2ev(i, k, eng):
+        def b2_out():
             nc.scalar.copy(out=b2bc[:], in_=ps["pb"][:])
 
-        def op_w1T(a, k, eng):
-            if a == 3:
-                pw = tps.tile([P, 256], F32, name="pw%d" % a, tag="t")
-            else:
-                pw = yps.tile([P, 256], F32, name="pw%d" % a, tag="y")
-            ps[("pw", a)] = pw
-            for u in range(2):
+        def w1_turn(a0, a1):
+            pw = yps.tile([P, (a1 - a0) * 256], F32, name="pw%d" % a0, tag="y")
+            ps[("pw", a0)] = pw
+            for k in range(2 * (a1 - a0)):
+                a, u = a0 + k // 2, k % 2
                 nc.tensor.transpose(
-                    out=pw[:, u * P:(u + 1) * P],
-                    in_=w1words[:, a * 256 + u * P:a * 256 + (u + 1) * P],
+                    out=pw[:, k * P:(k + 1) * P],
+                    in_=w1words[:, a * 256 + u:(a + 1) * 256:2],
                     identity=identf[:],
                 )
 
-        def op_w1ev(a, k, eng):
+        def w1_out(eng, a0, a1):
             copy_on(
                 eng,
-                w1gwords[:, a * 256:(a + 1) * 256].rearrange("q (m u) -> q m u", u=2),
-                ps[("pw", a)][:].rearrange("q (u m) -> q m u", u=2),
+                w1gwords[:, a0 * 256:a1 * 256].rearrange("q (a m u) -> q a m u", a=a1 - a0, u=2),
+                ps[("pw", a0)][:].rearrange("q (a u m) -> q a m u", a=a1 - a0, u=2),
             )
 
-        def op_w1q(a, k, eng):
+        def w1_quant(a0, a1):
             nc.vector.quantize_mx(
-                out=w1c[:, a * P:(a + 1) * P].bitcast(FP8X4),
-                scales=w1s[:, a * P:(a + 1) * P],
-                in_=w1g[:, a * 512:(a + 1) * 512],
+                out=w1c[:, a0 * P:a1 * P].bitcast(FP8X4),
+                scales=w1s[:, a0 * P:a1 * P],
+                in_=w1g[:, a0 * 512:a1 * 512],
             )
 
-        def op_xw(key, hf, eng):
-            n, ph = key // 2, key % 2
+        def x_weave(eng, n, ph, s0, s1):
             if n == 0:
-                dst = xg[hf][:, ph * 1024:(ph + 1) * 1024]
+                hf = s0 // 32
+                dst = xg[hf][:, ph * 1024 + (s0 - hf * 32) * 32:ph * 1024 + (s1 - hf * 32) * 32]
             else:
-                dst = xg[2 + ph][:, hf * 1024:(hf + 1) * 1024]
-            nc.vector.tensor_copy(
-                out=dst.rearrange("q (s i t) -> q s t i", s=32, i=8),
-                in_=xsb[n][:].rearrange("q (t s h i) -> q h s t i", t=4, h=2, i=8)[:, ph, hf * 32:(hf + 1) * 32],
-            )
-
-        def op_xe(hf, e, eng):
+                dst = xg[2 + ph][:, s0 * 32:s1 * 32]
             copy_on(
                 eng,
-                xg[hf][:, 1024 + e * 512:1024 + (e + 1) * 512].rearrange("q (s i t) -> q s t i", s=16, i=8),
-                xsb[0][:].rearrange("q (t s h i) -> q h s t i", t=4, h=2, i=8)[:, 1, hf * 32 + e * 16:hf * 32 + (e + 1) * 16],
+                dst.rearrange("q (s i t) -> q s t i", i=8, t=4),
+                xsb[n][:].rearrange("q (t s h i) -> q h s t i", t=4, h=2, i=8)[:, ph, s0:s1],
             )
 
-        def op_xq(k, z, eng):
+        def x_quant(k):
             nc.vector.quantize_mx(out=xc[k][:].bitcast(FP8X4), scales=xs[k][:], in_=xg[k][:])
 
-        def op_w2T(bb, z, eng):
+        def w2_turn(bb):
             pw2 = yps.tile([P, 512], F32, name="pw2x%d" % bb, tag="y")
             ps[("pw2", bb)] = pw2
             for k in range(4):
@@ -188,17 +145,17 @@ def tile_getspatialgatingweights_pa_kernel(tc, x_norm, w1_u, b1_u, w2, b2, out):
                     identity=identf[:],
                 )
 
-        def op_w2ev(bb, z, eng):
+        def w2_out(eng, bb):
             copy_on(
                 eng,
                 w2gwords[:, bb * 512:(bb + 1) * 512].rearrange("q (b m u) -> q b m u", b=2, u=2),
                 ps[("pw2", bb)][:].rearrange("q (b u m) -> q b m u", b=2, u=2),
             )
 
-        def op_w2q(i, k, eng):
+        def w2_quant():
             nc.vector.quantize_mx(out=w2c[:].bitcast(FP8X4), scales=w2s[:], in_=w2g[:])
 
-        def op_mx1(j, x, eng):
+        def mx1(j, x):
             n, a = j // 4, j % 4
             z = zps.tile([P, 512], F32, name="z%dx%d" % (j, x), tag="z")
             ps[("z", j, x)] = z
@@ -212,7 +169,7 @@ def tile_getspatialgatingweights_pa_kernel(tc, x_norm, w1_u, b1_u, w2, b2, out):
                 stop=True,
             )
 
-        def op_g(j, x, eng):
+        def gelu(j, x):
             a = j % 4
             nc.scalar.activation(
                 out=usb[j][:, x * 512:(x + 1) * 512],
@@ -226,43 +183,27 @@ def tile_getspatialgatingweights_pa_kernel(tc, x_norm, w1_u, b1_u, w2, b2, out):
             w0 = u * 256 + ph * P if j < 4 else ph * 256 + u * P
             return usb[j][:].bitcast(F32)[:, w0:w0 + P]
 
-        def op_tr(j, z, eng):
-            ut = tps.tile([P, 512], F32, name="ut%d" % j, tag="t")
-            ps[("ut", j)] = ut
-            for k in range(4):
-                nc.tensor.transpose(out=ut[:, k * P:(k + 1) * P], in_=u_words(j, k // 2, k % 2), identity=identf[:])
+        def u_turn(j, ph0, ph1):
+            ut = tps.tile([P, (ph1 - ph0) * 256], F32, name="ut%dx%d" % (j, ph0), tag="t")
+            ps[("ut", j, ph0)] = ut
+            for k in range(2 * (ph1 - ph0)):
+                nc.tensor.transpose(out=ut[:, k * P:(k + 1) * P], in_=u_words(j, ph0 + k // 2, k % 2), identity=identf[:])
 
-        def op_trh(j, ph, eng):
-            ut = tps.tile([P, 256], F32, name="ut%dx%d" % (j, ph), tag="t")
-            ps[("uth", j, ph)] = ut
-            for u in range(2):
-                nc.tensor.transpose(out=ut[:, u * P:(u + 1) * P], in_=u_words(j, ph, u), identity=identf[:])
-
-        def op_uev(j, z, eng):
+        def u_out(eng, j, ph0, ph1):
             copy_on(
                 eng,
-                ug[j][:].bitcast(F32).rearrange("p (h m u) -> p h m u", h=2, u=2),
-                ps[("ut", j)][:].rearrange("p (h u m) -> p h m u", h=2, u=2),
+                ug[j][:].bitcast(F32)[:, ph0 * 256:ph1 * 256].rearrange("p (h m u) -> p h m u", h=ph1 - ph0, u=2),
+                ps[("ut", j, ph0)][:].rearrange("p (h u m) -> p h m u", h=ph1 - ph0, u=2),
             )
 
-        def op_uevh(j, ph, eng):
-            copy_on(
-                eng,
-                ug[j][:].bitcast(F32)[:, ph * 256:(ph + 1) * 256].rearrange("p (m u) -> p m u", u=2),
-                ps[("uth", j, ph)][:].rearrange("p (u m) -> p m u", u=2),
-            )
-
-        def op_uq(j, z, eng):
-            nc.vector.quantize_mx(out=uc[j][:].bitcast(FP8X4), scales=us[j][:], in_=ug[j][:])
-
-        def op_uqh(j, ph, eng):
+        def u_quant(j, ph0, ph1):
             nc.vector.quantize_mx(
-                out=uc[j][:, ph * P:(ph + 1) * P].bitcast(FP8X4),
-                scales=us[j][:, ph * P:(ph + 1) * P],
-                in_=ug[j][:, ph * 512:(ph + 1) * 512],
+                out=uc[j][:, ph0 * P:ph1 * P].bitcast(FP8X4),
+                scales=us[j][:, ph0 * P:ph1 * P],
+                in_=ug[j][:, ph0 * 512:ph1 * 512],
             )
 
-        def op_mx2(j, ph, eng):
+        def mx2(j, ph):
             y = yps.tile([P, 512], F32, name="y%dx%d" % (j, ph), tag="y")
             ps[("y", j, ph)] = y
             nc.tensor.matmul_mx(
@@ -283,23 +224,79 @@ def tile_getspatialgatingweights_pa_kernel(tc, x_norm, w1_u, b1_u, w2, b2, out):
                 op=ALU.add,
             )
 
-        def op_yev(j, ph, eng):
-            y_add(j, ph, 0, 64)
-            done[j] = done.get(j, 0) + 1
-            if done[j] == 2:
-                nc.sync.dma_start(out=ov[j // 4, j % 4], in_=osb[j][:])
+        def store(j, s0, s1):
+            nc.sync.dma_start(out=ov[j // 4, j % 4][:, s0 * 16:s1 * 16], in_=osb[j][:, s0 * 16:s1 * 16])
 
-        def op_yevh(ph, half, eng):
-            y_add(7, ph, half * 32, (half + 1) * 32)
-            done[(7, half)] = done.get((7, half), 0) + 1
-            if done[(7, half)] == 2:
-                nc.sync.dma_start(out=ov[1, 3][:, half * 512:(half + 1) * 512], in_=osb[7][:, half * 512:(half + 1) * 512])
+        w1_turn(0, 1)
+        b2_spread()
+        x_weave("V", 0, 0, 0, 16)
+        x_weave("S", 0, 1, 0, 16)
+        w1_out("S", 0, 1)
+        b2_out()
+        x_weave("V", 0, 0, 16, 32)
+        x_weave("V", 0, 1, 16, 32)
+        w1_quant(0, 1)
+        x_quant(0)
+        nc.vector.tensor_copy(out=b1f[:], in_=b1bf[:])
+        mx1(0, 0)
+        x_weave("S", 0, 1, 32, 52)
+        x_weave("V", 0, 0, 32, 64)
+        x_weave("V", 0, 1, 52, 64)
+        gelu(0, 0)
+        w1_turn(1, 2)
+        w1_turn(2, 4)
+        x_quant(1)
+        mx1(0, 1)
+        w1_out("S", 1, 2)
+        w1_out("S", 2, 4)
+        w2_turn(0)
+        w2_turn(1)
+        w1_quant(1, 2)
+        w1_quant(2, 4)
+        gelu(0, 1)
+        mx1(1, 0)
+        mx1(1, 1)
+        u_turn(0, 0, 2)
+        w2_out("V", 0)
 
-        ops = {
-            "b1f": op_b1f, "b2mm": op_b2mm, "b2ev": op_b2ev, "w1T": op_w1T, "w1ev": op_w1ev, "w1q": op_w1q,
-            "xw": op_xw, "xe": op_xe, "xq": op_xq, "w2T": op_w2T, "w2ev": op_w2ev, "w2q": op_w2q,
-            "mx1": op_mx1, "g": op_g, "tr": op_tr, "trh": op_trh, "uev": op_uev, "uevh": op_uevh,
-            "uq": op_uq, "uqh": op_uqh, "mx2": op_mx2, "yev": op_yev, "yevh": op_yevh,
-        }
-        for name, i, k, eng in ORDER:
-            ops[name](i, k, eng)
+        def early_v(i):
+            if i == 1:
+                x_weave("V", 1, 0, 0, 32)
+                x_weave("V", 1, 0, 32, 64)
+                x_weave("V", 1, 1, 0, 32)
+                x_weave("V", 1, 1, 32, 64)
+                w2_quant()
+            if i == 2:
+                x_quant(2)
+                x_quant(3)
+
+        def early_s(i):
+            if i == 1:
+                w2_out("S", 1)
+
+        for i in range(1, SLABS + 3):
+            if 3 <= i:
+                mx2(i - 3, 0)
+                mx2(i - 3, 1)
+            if i < SLABS:
+                gelu(i, 0)
+                gelu(i, 1)
+            if 1 <= i <= SLABS:
+                u_out("S", i - 1, 0, 2)
+            early_s(i)
+            if 2 <= i < SLABS + 2:
+                u_quant(i - 2, 0, 2)
+            early_v(i)
+            if i + 1 < SLABS:
+                mx1(i + 1, 0)
+                mx1(i + 1, 1)
+            if i < SLABS:
+                u_turn(i, 0, 2)
+            if 3 <= i < SLABS + 2:
+                y_add(i - 3, 0, 0, 64)
+                y_add(i - 3, 1, 0, 64)
+                store(i - 3, 0, 64)
+        for s0 in (0, 32):
+            y_add(SLABS - 1, 0, s0, s0 + 32)
+            y_add(SLABS - 1, 1, s0, s0 + 32)
+            store(SLABS - 1, s0, s0 + 32)

@@ -20,9 +20,9 @@ def tile_getspatialgatingweights_pa_kernel(tc, x_norm, w1_u, b1_u, w2, b2, out):
     nc = tc.nc
     with ExitStack() as ctx:
         const = ctx.enter_context(tc.tile_pool(name="const", bufs=1))
-        zps = ctx.enter_context(tc.psum_pool(name="zps", bufs=2))
+        zps = ctx.enter_context(tc.psum_pool(name="zps", bufs=3))
         tps = ctx.enter_context(tc.psum_pool(name="tps", bufs=2))
-        yps = ctx.enter_context(tc.psum_pool(name="yps", bufs=4))
+        yps = ctx.enter_context(tc.psum_pool(name="yps", bufs=3))
         ctx.enter_context(tc.manual_schedule())
 
         xv = x_norm.rearrange("n (q t) d h w -> n q t (d h w)", t=4)
@@ -275,6 +275,8 @@ def tile_getspatialgatingweights_pa_kernel(tc, x_norm, w1_u, b1_u, w2, b2, out):
                 w2_out("S", 1)
 
         for i in range(1, SLABS + 3):
+            if i + 1 < SLABS:
+                mx1(i + 1, 0)
             if 3 <= i:
                 mx2(i - 3, 0)
                 mx2(i - 3, 1)
@@ -288,7 +290,6 @@ def tile_getspatialgatingweights_pa_kernel(tc, x_norm, w1_u, b1_u, w2, b2, out):
                 u_quant(i - 2, 0, 2)
             early_v(i)
             if i + 1 < SLABS:
-                mx1(i + 1, 0)
                 mx1(i + 1, 1)
             if i < SLABS:
                 u_turn(i, 0, 2)

@@ -31,11 +31,8 @@ def tile_getspatialgatingweights_pa_kernel(tc, x_norm, w1_u, b1_u, w2, b2, out):
         ov = out.rearrange("n (m a) d h w -> n a m (d h w)", a=4)
 
         identf = const.tile([P, P], F32, name="identf")
-        ones = const.tile([P, P], BF16, name="ones")
-        bz = const.tile([P, 512], BF16, name="bz")
-        b2bc = const.tile([P, 512], F32, name="b2bc")
+        b2bc = const.tile([P, 512], BF16, name="b2bc")
         b1bf = const.tile([P, 4], BF16, name="b1bf")
-        b1f = const.tile([P, 4], F32, name="b1f")
         warm = const.tile([P, 1], F32, name="warm")
         warm2 = const.tile([P, 1], F32, name="warm2")
         w1sb = const.tile([P, 2048], BF16, name="w1sb")
@@ -61,8 +58,6 @@ def tile_getspatialgatingweights_pa_kernel(tc, x_norm, w1_u, b1_u, w2, b2, out):
 
         nc.scalar.dma_start(out=w1sb[:, 0:512], in_=w1v[:, 0, :])
         nc.scalar.dma_start(out=b1bf[:], in_=b1_u.rearrange("(m a) -> m a", a=4))
-        nc.gpsimd.memset(bz[:], 0.0)
-        nc.scalar.dma_start(out=bz[0:1, :], in_=b2.rearrange("(o k) -> o k", o=1))
         load_x(0, 0, 256)
         load_x(0, 256, 512)
         load_x(0, 512, 1024)
@@ -70,7 +65,7 @@ def tile_getspatialgatingweights_pa_kernel(tc, x_norm, w1_u, b1_u, w2, b2, out):
         nc.sync.dma_start(out=w2sb[:].rearrange("m (b g) -> m b g", b=4), in_=w2v)
         load_x(1, 0, 512)
         load_x(1, 512, 1024)
-        nc.gpsimd.memset(ones[:], 1.0)
+        nc.sync.dma_start(out=b2bc[:], in_=b2.partition_broadcast(P))
         make_identity(nc, identf[:])
         nc.vector.memset(warm[:], 0.0)
         nc.scalar.activation(out=warm2[:], in_=warm[:], func=ACT.Gelu)
@@ -86,14 +81,6 @@ def tile_getspatialgatingweights_pa_kernel(tc, x_norm, w1_u, b1_u, w2, b2, out):
                 nc.scalar.copy(out=dst, in_=srcv)
             else:
                 nc.vector.tensor_copy(out=dst, in_=srcv)
-
-        def b2_spread():
-            pb = yps.tile([P, 512], F32, name="pb", tag="y")
-            ps["pb"] = pb
-            nc.tensor.matmul(out=pb[:], lhsT=ones[:], rhs=bz[:], start=True, stop=True)
-
-        def b2_out():
-            nc.scalar.copy(out=b2bc[:], in_=ps["pb"][:])
 
         def w1_turn(a0, a1):
             pw = yps.tile([P, (a1 - a0) * 256], F32, name="pw%d" % a0, tag="y")
@@ -175,7 +162,7 @@ def tile_getspatialgatingweights_pa_kernel(tc, x_norm, w1_u, b1_u, w2, b2, out):
                 out=usb[j][:, x * 512:(x + 1) * 512],
                 in_=ps[("z", j, x)][:],
                 func=ACT.Gelu,
-                bias=b1f[:, a:a + 1],
+                bias=b1bf[:, a:a + 1],
                 scale=1.0,
             )
 
@@ -228,20 +215,17 @@ def tile_getspatialgatingweights_pa_kernel(tc, x_norm, w1_u, b1_u, w2, b2, out):
             nc.sync.dma_start(out=ov[j // 4, j % 4][:, s0 * 16:s1 * 16], in_=osb[j][:, s0 * 16:s1 * 16])
 
         w1_turn(0, 1)
-        b2_spread()
+        w1_out("V", 0, 1)
+        w1_quant(0, 1)
         x_weave("V", 0, 0, 0, 16)
         x_weave("S", 0, 1, 0, 16)
-        w1_out("S", 0, 1)
-        b2_out()
         x_weave("V", 0, 0, 16, 32)
-        x_weave("V", 0, 1, 16, 32)
-        w1_quant(0, 1)
+        x_weave("S", 0, 1, 16, 32)
         x_quant(0)
-        nc.vector.tensor_copy(out=b1f[:], in_=b1bf[:])
         mx1(0, 0)
-        x_weave("S", 0, 1, 32, 52)
+        x_weave("S", 0, 1, 32, 60)
         x_weave("V", 0, 0, 32, 64)
-        x_weave("V", 0, 1, 52, 64)
+        x_weave("V", 0, 1, 60, 64)
         gelu(0, 0)
         w1_turn(1, 2)
         w1_turn(2, 4)

@@ -62,9 +62,8 @@ def tile_getspatialgatingweights_pa_kernel(tc, x_norm, w1_u, b1_u, w2, b2, out):
         load_x(0, 256, 512)
         load_x(0, 512, 1024)
         nc.sync.dma_start(out=w1sb[:, 512:2048].rearrange("m (a c) -> m a c", a=3), in_=w1v[:, 1:4, :])
+        load_x(1, 0, 1024)
         nc.sync.dma_start(out=w2sb[:].rearrange("m (b g) -> m b g", b=4), in_=w2v)
-        load_x(1, 0, 512)
-        load_x(1, 512, 1024)
         nc.sync.dma_start(out=b2bc[:], in_=b2.partition_broadcast(P))
         make_identity(nc, identf[:])
         nc.vector.memset(warm[:], 0.0)
@@ -233,29 +232,25 @@ def tile_getspatialgatingweights_pa_kernel(tc, x_norm, w1_u, b1_u, w2, b2, out):
         mx1(0, 1)
         w1_out("S", 1, 2)
         w1_out("S", 2, 4)
-        w2_turn(0)
-        w2_turn(1)
         w1_quant(1, 2)
         w1_quant(2, 4)
         gelu(0, 1)
         mx1(1, 0)
         mx1(1, 1)
         u_turn(0, 0, 2)
-        w2_out("V", 0)
 
         def early_v(i):
             if i == 1:
-                x_weave("V", 1, 0, 0, 32)
-                x_weave("V", 1, 0, 32, 64)
-                x_weave("V", 1, 1, 0, 32)
-                x_weave("V", 1, 1, 32, 64)
-                w2_quant()
+                x_weave("V", 1, 0, 0, 64)
+                x_weave("V", 1, 1, 0, 64)
             if i == 2:
                 x_quant(2)
                 x_quant(3)
+                w2_out("V", 0)
+                w2_quant()
 
         def early_s(i):
-            if i == 1:
+            if i == 2:
                 w2_out("S", 1)
 
         for i in range(1, SLABS + 3):
@@ -277,6 +272,9 @@ def tile_getspatialgatingweights_pa_kernel(tc, x_norm, w1_u, b1_u, w2, b2, out):
                 mx1(i + 1, 1)
             if i < SLABS:
                 u_turn(i, 0, 2)
+            if i == 1:
+                w2_turn(0)
+                w2_turn(1)
             if 3 <= i < SLABS + 2:
                 y_add(i - 3, 0, 0, 64)
                 y_add(i - 3, 1, 0, 64)

@@ -33,6 +33,7 @@ def tile_getspatialgatingweights_pa_kernel(tc, x_norm, w1_u, b1_u, w2, b2, out):
         identf = const.tile([P, P], F32, name="identf")
         b2bc = const.tile([P, 512], BF16, name="b2bc")
         b1bf = const.tile([P, 4], BF16, name="b1bf")
+        idle = const.tile([P, 512], BF16, name="idle")
         warm = const.tile([P, 1], F32, name="warm")
         warm2 = const.tile([P, 1], F32, name="warm2")
         w1sb = const.tile([P, 2048], BF16, name="w1sb")
@@ -65,6 +66,7 @@ def tile_getspatialgatingweights_pa_kernel(tc, x_norm, w1_u, b1_u, w2, b2, out):
         load_x(1, 0, 1024)
         nc.sync.dma_start(out=w2sb[:].rearrange("m (b g) -> m b g", b=4), in_=w2v)
         nc.sync.dma_start(out=b2bc[:], in_=b2.partition_broadcast(P))
+        nc.gpsimd.memset(idle[:], 0.0)
         make_identity(nc, identf[:])
         nc.vector.memset(warm[:], 0.0)
         nc.scalar.activation(out=warm2[:], in_=warm[:], func=ACT.Gelu)
@@ -80,6 +82,10 @@ def tile_getspatialgatingweights_pa_kernel(tc, x_norm, w1_u, b1_u, w2, b2, out):
                 nc.scalar.copy(out=dst, in_=srcv)
             else:
                 nc.vector.tensor_copy(out=dst, in_=srcv)
+
+        def keep_warm(n):
+            for k in range(n):
+                nc.tensor.matmul(out=ps["idle"][:], lhsT=idle[:, 0:P], rhs=idle[:], start=True, stop=True)
 
         def w1_turn(a0, a1):
             pw = yps.tile([P, (a1 - a0) * 256], F32, name="pw%d" % a0, tag="y")
@@ -213,7 +219,10 @@ def tile_getspatialgatingweights_pa_kernel(tc, x_norm, w1_u, b1_u, w2, b2, out):
         def store(j, s0, s1):
             nc.sync.dma_start(out=ov[j // 4, j % 4][:, s0 * 16:s1 * 16], in_=osb[j][:, s0 * 16:s1 * 16])
 
+        ps["idle"] = tps.tile([P, 512], F32, name="idleps", tag="t")
+        keep_warm(5)
         w1_turn(0, 1)
+        keep_warm(3)
         w1_out("V", 0, 1)
         w1_quant(0, 1)
         x_weave("V", 0, 0, 0, 16)
@@ -222,6 +231,7 @@ def tile_getspatialgatingweights_pa_kernel(tc, x_norm, w1_u, b1_u, w2, b2, out):
         x_weave("S", 0, 1, 16, 32)
         x_quant(0)
         mx1(0, 0)
+        keep_warm(2)
         x_weave("S", 0, 1, 32, 60)
         x_weave("V", 0, 0, 32, 64)
         x_weave("V", 0, 1, 60, 64)

@@ -87,6 +87,10 @@ def tile_getspatialgatingweights_pa_kernel(tc, x_norm, w1_u, b1_u, w2, b2, out):
             for k in range(n):
                 nc.tensor.matmul(out=ps["idle"][:], lhsT=idle[:, 0:P], rhs=idle[:], start=True, stop=True)
 
+        def keep_warm_when_x_lands(n):
+            for k in range(n):
+                nc.tensor.matmul(out=ps["idle"][:, 0:256], lhsT=idle[:, 0:P], rhs=xsb[0][:, 256:512], start=True, stop=True)
+
         def w1_turn(a0, a1):
             pw = yps.tile([P, (a1 - a0) * 256], F32, name="pw%d" % a0, tag="y")
             ps[("pw", a0)] = pw
@@ -229,6 +233,7 @@ def tile_getspatialgatingweights_pa_kernel(tc, x_norm, w1_u, b1_u, w2, b2, out):
         x_weave("S", 0, 1, 0, 16)
         x_weave("V", 0, 0, 16, 32)
         x_weave("S", 0, 1, 16, 32)
+        keep_warm_when_x_lands(4)
         x_quant(0)
         mx1(0, 0)
         keep_warm(2)

from contextlib import ExitStack

import concourse.mybir as mybir
from concourse.masks import make_identity

F32 = mybir.dt.float32
BF16 = mybir.dt.bfloat16
U32 = mybir.dt.uint32
U8 = mybir.dt.uint8
FP8X4 = mybir.dt.float8_e4m3fn_x4
ACT = mybir.ActivationFunctionType
ALU = mybir.AluOpType

P = 128
FLOPS = 2 * 2 * 512 * 512 * 1024 * 2
SLABS = 8


def tile_getspatialgatingweights_pa_kernel(tc, x_norm, w1_u, b1_u, w2, b2, out):
    nc = tc.nc
    with ExitStack() as ctx:
        const = ctx.enter_context(tc.tile_pool(name="const", bufs=1))
        zps = ctx.enter_context(tc.psum_pool(name="zps", bufs=3))
        tps = ctx.enter_context(tc.psum_pool(name="tps", bufs=2))
        yps = ctx.enter_context(tc.psum_pool(name="yps", bufs=3))
        ctx.enter_context(tc.manual_schedule())

        xv = x_norm.rearrange("n (q t) d h w -> n q t (d h w)", t=4)
        w1v = w1_u.rearrange("(m a) c -> m a c", a=4)
        w2v = w2.rearrange("(b m) g -> m b g", m=P)
        ov = out.rearrange("n (m a) d h w -> n a m (d h w)", a=4)

        identf = const.tile([P, P], F32, name="identf")
        b2bc = const.tile([P, 512], BF16, name="b2bc")
        b1bf = const.tile([P, 4], BF16, name="b1bf")
        idle = const.tile([P, 512], BF16, name="idle")
        warm = const.tile([P, 1], F32, name="warm")
        warm2 = const.tile([P, 1], F32, name="warm2")
        w1sb = const.tile([P, 2048], BF16, name="w1sb")
        w2sb = const.tile([P, 2048], BF16, name="w2sb")
        w1g = const.tile([P, 2048], BF16, name="w1g", align_bytes=64)
        w2g = const.tile([P, 2048], BF16, name="w2g", align_bytes=64)
        w1c = const.tile([P, 512], U32, name="w1c", align_bytes=64)
        w1s = const.tile([P, 512], U8, name="w1s", align_bytes=64)
        w2c = const.tile([P, 512], U32, name="w2c", align_bytes=64)
        w2s = const.tile([P, 512], U8, name="w2s", align_bytes=64)
        xsb = [const.tile([P, 4096], BF16, name="xsb%d" % n) for n in range(2)]
        xg = [const.tile([P, 2048], BF16, name="xg%d" % k, align_bytes=64) for k in range(4)]
        xc = [const.tile([P, 512], U32, name="xc%d" % k, align_bytes=64) for k in range(4)]
        xs = [const.tile([P, 512], U8, name="xs%d" % k, align_bytes=64) for k in range(4)]
        usb = [const.tile([P, 1024], BF16, name="usb%d" % j) for j in range(SLABS)]
        ug = [const.tile([P, 1024], BF16, name="ug%d" % j, align_bytes=64) for j in range(SLABS)]
        uc = [const.tile([P, 256], U32, name="uc%d" % j, align_bytes=64) for j in range(SLABS)]
        us = [const.tile([P, 256], U8, name="us%d" % j, align_bytes=64) for j in range(SLABS)]
        osb = [const.tile([P, 1024], F32, name="osb%d" % j) for j in range(SLABS)]

        def load_x(n, v0, v1):
            nc.sync.dma_start(out=xsb[n][:].rearrange("q (t v) -> q t v", t=4)[:, :, v0:v1], in_=xv[n][:, :, v0:v1])

        nc.scalar.dma_start(out=w1sb[:, 0:512], in_=w1v[:, 0, :])
        nc.scalar.dma_start(out=b1bf[:], in_=b1_u.rearrange("(m a) -> m a", a=4))
        load_x(0, 0, 256)
        load_x(0, 256, 512)
        load_x(0, 512, 1024)
        nc.sync.dma_start(out=w1sb[:, 512:2048].rearrange("m (a c) -> m a c", a=3), in_=w1v[:, 1:4, :])
        load_x(1, 0, 1024)
        nc.sync.dma_start(out=w2sb[:].rearrange("m (b g) -> m b g", b=4), in_=w2v)
        nc.sync.dma_start(out=b2bc[:], in_=b2.partition_broadcast(P))
        nc.gpsimd.memset(idle[:], 0.0)
        make_identity(nc, identf[:])
        nc.vector.memset(warm[:], 0.0)
        nc.scalar.activation(out=warm2[:], in_=warm[:], func=ACT.Gelu)

        w1words = w1sb[:].bitcast(F32)
        w1gwords = w1g[:].bitcast(F32)
        w2words = w2sb[:].bitcast(F32)
        w2gwords = w2g[:].bitcast(F32)
        ps = {}

        def copy_on(eng, dst, srcv):
            if eng == "S":
                nc.scalar.copy(out=dst, in_=srcv)
            else:
                nc.vector.tensor_copy(out=dst, in_=srcv)

        def keep_warm(n):
            for k in range(n):
                nc.tensor.matmul(out=ps["idle"][:], lhsT=idle[:, 0:P], rhs=idle[:], start=True, stop=True)

        def keep_warm_when_x_lands(n):
            for k in range(n):
                nc.tensor.matmul(out=ps["idle"][:, 0:256], lhsT=idle[:, 0:P], rhs=xsb[0][:, 256:512], start=True, stop=True)

        def w1_turn(a0, a1):
            pw = yps.tile([P, (a1 - a0) * 256], F32, name="pw%d" % a0, tag="y")
            ps[("pw", a0)] = pw
            for k in range(2 * (a1 - a0)):
                a, u = a0 + k // 2, k % 2
                nc.tensor.transpose(
                    out=pw[:, k * P:(k + 1) * P],
                    in_=w1words[:, a * 256 + u:(a + 1) * 256:2],
                    identity=identf[:],
                )

        def w1_out(eng, a0, a1):
            copy_on(
                eng,
                w1gwords[:, a0 * 256:a1 * 256].rearrange("q (a m u) -> q a m u", a=a1 - a0, u=2),
                ps[("pw", a0)][:].rearrange("q (a u m) -> q a m u", a=a1 - a0, u=2),
            )

        def w1_quant(a0, a1):
            nc.vector.quantize_mx(
                out=w1c[:, a0 * P:a1 * P].bitcast(FP8X4),
                scales=w1s[:, a0 * P:a1 * P],
                in_=w1g[:, a0 * 512:a1 * 512],
            )

        def x_weave(eng, n, ph, s0, s1):
            if n == 0:
                hf = s0 // 32
                dst = xg[hf][:, ph * 1024 + (s0 - hf * 32) * 32:ph * 1024 + (s1 - hf * 32) * 32]
            else:
                dst = xg[2 + ph][:, s0 * 32:s1 * 32]
            copy_on(
                eng,
                dst.rearrange("q (s i t) -> q s t i", i=8, t=4),
                xsb[n][:].rearrange("q (t s h i) -> q h s t i", t=4, h=2, i=8)[:, ph, s0:s1],
            )

        def x_quant(k):
            nc.vector.quantize_mx(out=xc[k][:].bitcast(FP8X4), scales=xs[k][:], in_=xg[k][:])

        def w2_turn(bb):
            pw2 = yps.tile([P, 512], F32, name="pw2x%d" % bb, tag="y")
            ps[("pw2", bb)] = pw2
            for k in range(4):
                nc.tensor.transpose(
                    out=pw2[:, k * P:(k + 1) * P],
                    in_=w2words[:, bb * 512 + k * P:bb * 512 + (k + 1) * P],
                    identity=identf[:],
                )

        def w2_out(eng, bb):
            copy_on(
                eng,
                w2gwords[:, bb * 512:(bb + 1) * 512].rearrange("q (b m u) -> q b m u", b=2, u=2),
                ps[("pw2", bb)][:].rearrange("q (b u m) -> q b m u", b=2, u=2),
            )

        def w2_quant():
            nc.vector.quantize_mx(out=w2c[:].bitcast(FP8X4), scales=w2s[:], in_=w2g[:])

        def mx1(j, x):
            n, a = j // 4, j % 4
            z = zps.tile([P, 512], F32, name="z%dx%d" % (j, x), tag="z")
            ps[("z", j, x)] = z
            nc.tensor.matmul_mx(
                out=z[:],
                lhsT=w1c[:, a * P:(a + 1) * P].bitcast(FP8X4),
                lhsT_scale=w1s[:, a * P:(a + 1) * P],
                rhs=xc[2 * n + x][:].bitcast(FP8X4),
                rhs_scale=xs[2 * n + x][:],
                start=True,
                stop=True,
            )

        def gelu(j, x):
            a = j % 4
            nc.scalar.activation(
                out=usb[j][:, x * 512:(x + 1) * 512],
                in_=ps[("z", j, x)][:],
                func=ACT.Gelu,
                bias=b1bf[:, a:a + 1],
                scale=1.0,
            )

        def u_words(j, ph, u):
            w0 = u * 256 + ph * P if j < 4 else ph * 256 + u * P
            return usb[j][:].bitcast(F32)[:, w0:w0 + P]

        def u_turn(j, ph0, ph1):
            ut = tps.tile([P, (ph1 - ph0) * 256], F32, name="ut%dx%d" % (j, ph0), tag="t")
            ps[("ut", j, ph0)] = ut
            for k in range(2 * (ph1 - ph0)):
                nc.tensor.transpose(out=ut[:, k * P:(k + 1) * P], in_=u_words(j, ph0 + k // 2, k % 2), identity=identf[:])

        def u_out(eng, j, ph0, ph1):
            copy_on(
                eng,
                ug[j][:].bitcast(F32)[:, ph0 * 256:ph1 * 256].rearrange("p (h m u) -> p h m u", h=ph1 - ph0, u=2),
                ps[("ut", j, ph0)][:].rearrange("p (h u m) -> p h m u", h=ph1 - ph0, u=2),
            )

        def u_quant(j, ph0, ph1):
            nc.vector.quantize_mx(
                out=uc[j][:, ph0 * P:ph1 * P].bitcast(FP8X4),
                scales=us[j][:, ph0 * P:ph1 * P],
                in_=ug[j][:, ph0 * 512:ph1 * 512],
            )

        def mx2(j, ph):
            y = yps.tile([P, 512], F32, name="y%dx%d" % (j, ph), tag="y")
            ps[("y", j, ph)] = y
            nc.tensor.matmul_mx(
                out=y[:],
                lhsT=uc[j][:, ph * P:(ph + 1) * P].bitcast(FP8X4),
                lhsT_scale=us[j][:, ph * P:(ph + 1) * P],
                rhs=w2c[:].bitcast(FP8X4),
                rhs_scale=w2s[:],
                start=True,
                stop=True,
            )

        def y_add(j, ph, s0, s1):
            nc.vector.tensor_tensor(
                out=osb[j][:].rearrange("m (s h i) -> m h s i", h=2, i=8)[:, ph, s0:s1],
                in0=ps[("y", j, ph)][:].rearrange("m (s i) -> m s i", i=8)[:, s0:s1],
                in1=b2bc[:].rearrange("m (s i) -> m s i", i=8)[:, s0:s1],
                op=ALU.add,
            )

        def store(j, s0, s1):
            nc.sync.dma_start(out=ov[j // 4, j % 4][:, s0 * 16:s1 * 16], in_=osb[j][:, s0 * 16:s1 * 16])

        ps["idle"] = tps.tile([P, 512], F32, name="idleps", tag="t")
        keep_warm(5)
        w1_turn(0, 1)
        keep_warm(3)
        w1_out("V", 0, 1)
        w1_quant(0, 1)
        x_weave("V", 0, 0, 0, 16)
        x_weave("S", 0, 1, 0, 16)
        x_weave("V", 0, 0, 16, 32)
        x_weave("S", 0, 1, 16, 32)
        keep_warm_when_x_lands(4)
        x_quant(0)
        mx1(0, 0)
        keep_warm(2)
        x_weave("S", 0, 1, 32, 60)
        x_weave("V", 0, 0, 32, 64)
        x_weave("V", 0, 1, 60, 64)
        gelu(0, 0)
        w1_turn(1, 2)
        w1_turn(2, 4)
        x_quant(1)
        mx1(0, 1)
        w1_out("S", 1, 2)
        w1_out("S", 2, 4)
        w1_quant(1, 2)
        w1_quant(2, 4)
        gelu(0, 1)
        mx1(1, 0)
        mx1(1, 1)
        u_turn(0, 0, 2)

        def early_v(i):
            if i == 1:
                x_weave("V", 1, 0, 0, 64)
                x_weave("V", 1, 1, 0, 64)
            if i == 2:
                x_quant(2)
                x_quant(3)
                w2_out("V", 0)
                w2_quant()

        def early_s(i):
            if i == 2:
                w2_out("S", 1)

        for i in range(1, SLABS + 3):
            if i + 1 < SLABS:
                mx1(i + 1, 0)
            if 3 <= i:
                mx2(i - 3, 0)
                mx2(i - 3, 1)
            if i < SLABS:
                gelu(i, 0)
                gelu(i, 1)
            if 1 <= i <= SLABS:
                u_out("S", i - 1, 0, 2)
            early_s(i)
            if 2 <= i < SLABS + 2:
                u_quant(i - 2, 0, 2)
            early_v(i)
            if i + 1 < SLABS:
                mx1(i + 1, 1)
            if i < SLABS:
                u_turn(i, 0, 2)
            if i == 1:
                w2_turn(0)
                w2_turn(1)
            if 3 <= i < SLABS + 2:
                y_add(i - 3, 0, 0, 64)
                y_add(i - 3, 1, 0, 64)
                store(i - 3, 0, 64)
        for s0 in (0, 32):
            y_add(SLABS - 1, 0, s0, s0 + 32)
            y_add(SLABS - 1, 1, s0, s0 + 32)
            store(SLABS - 1, s0, s0 + 32)
